import numpy as np
import ml_dtypes


def mxq(x, axis, fmt="e4m3"):
    dtype, down = {"e4m3": (ml_dtypes.float8_e4m3fn, 7), "e5m2": (ml_dtypes.float8_e5m2, 14)}[fmt]
    v = np.moveaxis(np.asarray(x, np.float32).astype(ml_dtypes.bfloat16).astype(np.float64), axis, -1)
    blocks = v.reshape(v.shape[:-1] + (-1, 32))
    amax = np.abs(blocks).max(-1, keepdims=True)
    byte = np.maximum(np.where(amax > 0, np.frexp(amax)[1] - 1 + 127, 0) - down, 1)
    scale = np.exp2(byte - 127.0)
    codes = (blocks / scale).astype(np.float32).astype(dtype).astype(np.float64)
    return np.moveaxis((codes * scale).reshape(v.shape), -1, axis)


WIDE = False


def mx_kscale(k):
    if not WIDE:
        return np.ones(k)
    levels = np.array([10, -10, 5, -5, 0])
    a = np.random.permutation(np.resize(levels, k // 512 * 4)).reshape(k // 512, 4)
    idx = np.arange(k)
    return np.exp2(a[idx // 512, idx % 128 // 32])


BF16 = ml_dtypes.bfloat16


def bf(x):
    return np.asarray(x, np.float32).astype(BF16)


def f64(x):
    return np.asarray(x).astype(np.float64)


B, S, D, P, PW, L = 2, 256, 1024, 4, 2, 2
K = P * D
EPS = 1e-5


def layer_norm(v, g, b):
    m = v.mean(-1, keepdims=True)
    var = np.square(v - m).mean(-1, keepdims=True)
    return (v - m) * (1.0 / np.sqrt(var + EPS)) * g + b


def setup_inputs():
    n = np.random.standard_normal
    s = mx_kscale(K)
    return {"e": bf(n((B, S, K)) * 0.8 * s),
            "h": bf(n((B, S, D)) * 0.8 + 0.3),
            "ent_pw": bf(n((K, D)) / np.sqrt(K) / s[:, None]),
            "ent_pb": bf(n(D) * 0.2),
            "ln3_g": bf(1.0 + 0.1 * n(D)),
            "ln3_b": bf(0.2 * n(D) + 0.2),
            "path_w": bf(n((PW, D, D)) * 0.7 / np.sqrt(D)),
            "path_b": bf(n((PW, D)) * 0.2),
            "phase": bf(n((PW, D))),
            "ln4_g": bf(1.0 + 0.1 * n(D)),
            "ln4_b": bf(0.2 * n(D))}


def reference(e, h, ent_pw, ent_pb, ln3_g, ln3_b, path_w, path_b, phase, ln4_g, ln4_b):
    ent = (mxq(f64(e), 2, "e4m3") @ mxq(f64(ent_pw), 0, "e4m3")) + f64(ent_pb)
    hn = layer_norm(f64(h) + ent, f64(ln3_g), f64(ln3_b))
    t = (mxq(hn, 2, "e4m3")[None] @ mxq(f64(path_w), 1, "e4m3")[:, None]) + f64(path_b)[:, None, None, :]
    mod = np.cos(f64(phase)) + np.sin(f64(phase))
    interf = np.sum(t * mod[:, None, None, :], axis=0)
    return layer_norm(hn + interf, f64(ln4_g), f64(ln4_b))

@@ -1,0 +1,370 @@
+from contextlib import ExitStack
+import math
+
+import concourse.mybir as mybir
+from concourse.masks import make_identity
+
+F32 = mybir.dt.float32
+BF16 = mybir.dt.bfloat16
+I32 = mybir.dt.int32
+U32 = mybir.dt.uint32
+U8 = mybir.dt.uint8
+FP8X4 = mybir.dt.float8_e4m3fn_x4
+ALU = mybir.AluOpType
+ACT = mybir.ActivationFunctionType
+
+P = 128
+PACK = 4
+K_PASS = P * PACK
+BANK = 512
+
+TOKENS = 512
+TOKEN_TILES = TOKENS // P
+FEATURES = 1024
+FEATURE_TILES = FEATURES // P
+HALVES = FEATURES // BANK
+K_ENT = 4096
+ENT_PASSES = K_ENT // K_PASS
+PATHS = 2
+PATH_PASSES = FEATURES // K_PASS
+GROUP_TILES = 2
+GROUP = GROUP_TILES * P
+EPS = 1e-5
+
+ENT_VECTOR_COLS = 512
+PATH_VECTOR_COLS = 256
+
+TWO_PI_HEAD = 6.28125
+TWO_PI_REST = 2.0 * math.pi - TWO_PI_HEAD
+ROUND_TO_INT = 12582912.0
+
+FLOPS = 2 * TOKENS * K_ENT * FEATURES + 2 * PATHS * TOKENS * FEATURES * FEATURES
+
+
+def tile_quantuminspiredneuralcore_pb_kernel(
+    tc, e, h, ent_pw, ent_pb, ln3_g, ln3_b, path_w, path_b, phase, ln4_g, ln4_b, out
+):
+    nc = tc.nc
+    e_rows = e.flatten_outer_dims()
+    h_rows = h.flatten_outer_dims()
+    out_rows = out.flatten_outer_dims()
+
+    with ExitStack() as ctx:
+        ctx.enter_context(tc.manual_schedule())
+        consts = ctx.enter_context(tc.tile_pool(name="consts", bufs=1))
+        keep = ctx.enter_context(tc.tile_pool(name="keep", bufs=1))
+        stats = ctx.enter_context(tc.tile_pool(name="stats", bufs=TOKEN_TILES))
+        scratch = ctx.enter_context(tc.tile_pool(name="scratch", bufs=2))
+        stage = ctx.enter_context(tc.tile_pool(name="stage", bufs=4))
+        psum = ctx.enter_context(tc.psum_pool(name="psum", bufs=8))
+
+        def zeroed_rows(name):
+            rows = consts.tile([P, FEATURES], BF16, name=name)
+            nc.vector.memset(rows[:].bitcast(I32), 0)
+            return rows
+
+        def spread_row(rows, r, name):
+            pick_row = ident_bf16[:, r : r + 1].to_broadcast([P, P])
+            bank = psum.tile([P, FEATURES], BF16, tag="bank")
+            for half in range(HALVES):
+                cols = slice(half * BANK, (half + 1) * BANK)
+                nc.tensor.matmul(out=bank[:, cols], lhsT=pick_row, rhs=rows[:, cols], start=True, stop=True)
+            spread = consts.tile([P, FEATURES], BF16, name=name)
+            nc.scalar.copy(out=spread[:], in_=bank[:])
+            return spread
+
+        def load_and_regroup(rows_by_slot, vector_cols):
+            raw = stage.tile([P, PACK * FEATURES], BF16, tag="raw")
+            nc.sync.dma_start(out=raw[:].rearrange("p (a b) -> p a b", a=rows_by_slot.shape[1]), in_=rows_by_slot)
+            grouped = stage.tile([P, FEATURES, PACK], BF16, tag="grouped", align_bytes=64)
+            src = raw[:].rearrange("p (t c i) -> p c t i", t=PACK, i=4)
+            dst = grouped[:].rearrange("p (c i) t -> p c t i", i=4)
+            split = vector_cols // 4
+            nc.vector.tensor_copy(out=dst[:, :split], in_=src[:, :split])
+            nc.scalar.copy(out=dst[:, split:], in_=src[:, split:])
+            return grouped
+
+        def quantise_weight(grouped, codes, scales):
+            nc.vector.quantize_mx(
+                out=codes.bitcast(FP8X4), scales=scales, in_=grouped[:].rearrange("p n t -> p (n t)")
+            )
+
+        def add_and_mean(dst, banks, addend):
+            sums = stats.tile([P, HALVES], F32)
+            for half in range(HALVES):
+                cols = slice(half * BANK, (half + 1) * BANK)
+                nc.vector.scalar_tensor_tensor(
+                    out=dst[:, cols], in0=banks[half][:], scalar=0.0, in1=addend[:, cols],
+                    op0=ALU.add, op1=ALU.add, accum_out=sums[:, half : half + 1],
+                )
+            neg_mean = stats.tile([P, 1], F32)
+            nc.vector.tensor_scalar(
+                out=neg_mean[:], in0=sums[:, 0:1], scalar1=sums[:, 1:2], scalar2=-1.0 / FEATURES,
+                op0=ALU.add, op1=ALU.mult,
+            )
+            return neg_mean
+
+        def deviation(src, neg_mean):
+            squares = scratch.tile([P, FEATURES], BF16)
+            sum_sq = stats.tile([P, 1], F32)
+            nc.scalar.activation(
+                out=squares[:], in_=src, func=ACT.Square, bias=neg_mean[:], scale=1.0, accum_out=sum_sq[:]
+            )
+            std = stats.tile([P, 1], F32)
+            nc.scalar.activation(out=std[:], in_=sum_sq[:], func=ACT.Sqrt, bias=eps[:], scale=1.0 / FEATURES)
+            return std
+
+        def centre_and_gain(dst, src, neg_mean, gain):
+            nc.vector.scalar_tensor_tensor(out=dst, in0=src, scalar=neg_mean[:], in1=gain, op0=ALU.add, op1=ALU.mult)
+
+        def divide_and_shift(dst, std, shift):
+            rstd = stats.tile([P, 1], F32)
+            nc.vector.reciprocal(out=rstd[:], in_=std[:])
+            nc.vector.scalar_tensor_tensor(out=dst, in0=dst, scalar=rstd[:], in1=shift, op0=ALU.mult, op1=ALU.add)
+
+        ident_f32 = consts.tile([P, P], F32)
+        make_identity(nc, ident_f32[:])
+        early_rows = zeroed_rows("early_rows")
+        vec_rows = zeroed_rows("vec_rows")
+        eps = consts.tile([P, 1], F32)
+        nc.vector.memset(eps[:], EPS)
+        ident_bf16 = consts.tile([P, P], BF16)
+        nc.vector.tensor_copy(out=ident_bf16[:], in_=ident_f32[:])
+
+        h_sb = keep.tile([P, TOKEN_TILES, FEATURES], BF16)
+        e_raw = [stage.tile([P, K_ENT], BF16, tag="raw", name="e_raw_%d" % tt) for tt in range(TOKEN_TILES)]
+        nc.scalar.dma_start(out=early_rows[0:1, :], in_=ent_pb.unsqueeze(0))
+        nc.scalar.dma_start(out=vec_rows[0:1, :], in_=ln3_g.unsqueeze(0))
+        nc.scalar.dma_start(out=vec_rows[1:2, :], in_=ln3_b.unsqueeze(0))
+        nc.scalar.dma_start(out=vec_rows[2:4, :], in_=path_b)
+        nc.scalar.dma_start(out=vec_rows[4:6, :], in_=phase)
+        nc.sync.dma_start(out=h_sb[:], in_=h_rows.rearrange("(t p) f -> p t f", p=P))
+        for tt in range(TOKEN_TILES):
+            nc.sync.dma_start(out=e_raw[tt][:], in_=e_rows[tt * P : (tt + 1) * P, :])
+        table_warm = consts.tile([P, 1], F32)
+        nc.scalar.activation(out=table_warm[:], in_=eps[:], func=ACT.Sin)
+
+        x_all = keep.tile([P, TOKEN_TILES, FEATURES], F32)
+        hn_all = keep.tile([P, TOKEN_TILES, FEATURES], F32)
+        hn_grouped = keep.tile([P, PATH_PASSES, TOKENS, PACK], BF16, align_bytes=64)
+        hn_codes = keep.tile([P, PATH_PASSES, TOKENS], U32, align_bytes=64)
+        hn_scales = keep.tile([P, PATH_PASSES, TOKENS], U8, align_bytes=64)
+        w2_codes = keep.tile([P, PATHS, PATH_PASSES, FEATURES], U32, align_bytes=64)
+        w2_scales = keep.tile([P, PATHS, PATH_PASSES, FEATURES], U8, align_bytes=64)
+
+        ent_pb_spread = spread_row(early_rows, 0, "ent_pb_spread")
+        ln3_g_spread = spread_row(vec_rows, 0, "ln3_g_spread")
+        ln3_b_spread = spread_row(vec_rows, 1, "ln3_b_spread")
+
+        cols_bank = psum.tile([P, FEATURE_TILES, P], BF16, tag="bank")
+        for j in range(FEATURE_TILES):
+            nc.tensor.transpose(cols_bank[:, j, :], vec_rows[:, j * P : (j + 1) * P], ident_bf16[:])
+        path_b_cols = consts.tile([P, PATHS, FEATURE_TILES], F32)
+        nc.vector.tensor_copy(out=path_b_cols[:], in_=cols_bank[:, :, 2:4].rearrange("p j r -> p r j"))
+        phase_cols = consts.tile([P, PATHS, FEATURE_TILES], F32)
+        nc.vector.tensor_copy(out=phase_cols[:], in_=cols_bank[:, :, 4:6].rearrange("p j r -> p r j"))
+
+        turns = consts.tile([P, PATHS, FEATURE_TILES], F32)
+        nc.vector.tensor_scalar(
+            out=turns[:], in0=phase_cols[:], scalar1=1.0 / (2.0 * math.pi), scalar2=ROUND_TO_INT,
+            op0=ALU.mult, op1=ALU.add,
+        )
+        nc.vector.tensor_scalar(out=turns[:], in0=turns[:], scalar1=ROUND_TO_INT, scalar2=None, op0=ALU.subtract)
+        angle = consts.tile([P, PATHS, FEATURE_TILES], F32)
+        nc.vector.scalar_tensor_tensor(
+            out=angle[:], in0=turns[:], scalar=-TWO_PI_HEAD, in1=phase_cols[:], op0=ALU.mult, op1=ALU.add
+        )
+        nc.vector.scalar_tensor_tensor(
+            out=angle[:], in0=turns[:], scalar=-TWO_PI_REST, in1=angle[:], op0=ALU.mult, op1=ALU.add
+        )
+        sin_full = consts.tile([P, PATHS, FEATURE_TILES], F32)
+        nc.scalar.activation(out=sin_full[:], in_=angle[:], func=ACT.Sin)
+        sin_half = consts.tile([P, PATHS, FEATURE_TILES], F32)
+        nc.scalar.activation(out=sin_half[:], in_=angle[:], func=ACT.Sin, scale=0.5)
+
+        for tt in range(TOKEN_TILES):
+            nc.vector.tensor_tensor(out=x_all[:, tt, :], in0=h_sb[:, tt, :], in1=ent_pb_spread[:], op=ALU.add)
+
+        mod = consts.tile([P, PATHS, FEATURE_TILES], F32)
+        nc.vector.tensor_tensor(out=mod[:], in0=sin_half[:], in1=sin_half[:], op=ALU.mult)
+        nc.vector.tensor_scalar(out=mod[:], in0=mod[:], scalar1=-2.0, scalar2=1.0, op0=ALU.mult, op1=ALU.add)
+        nc.vector.tensor_tensor(out=mod[:], in0=mod[:], in1=sin_full[:], op=ALU.add)
+        bias_mod = consts.tile([P, PATHS, FEATURE_TILES], F32)
+        nc.vector.tensor_tensor(out=bias_mod[:], in0=path_b_cols[:], in1=mod[:], op=ALU.mult)
+        bias_sum = consts.tile([P, FEATURE_TILES], F32)
+        nc.vector.tensor_tensor(out=bias_sum[:], in0=bias_mod[:, 0, :], in1=bias_mod[:, 1, :], op=ALU.add)
+
+        with tc.tile_pool(name="stage1", bufs=1) as stage1:
+            e_codes = stage1.tile([P, TOKEN_TILES, ENT_PASSES, P], U32, align_bytes=64)
+            e_scales = stage1.tile([P, TOKEN_TILES, ENT_PASSES, P], U8, align_bytes=64)
+            w1_codes = stage1.tile([P, ENT_PASSES, FEATURES], U32, align_bytes=64)
+            w1_scales = stage1.tile([P, ENT_PASSES, FEATURES], U8, align_bytes=64)
+            chunks = []
+            for c in range(ENT_PASSES):
+                rows = ent_pw[c * K_PASS : (c + 1) * K_PASS, :].rearrange("(u p s) n -> p u (s n)", u=2, s=2)
+                chunks.append((rows, ENT_VECTOR_COLS, w1_codes[:, c, :], w1_scales[:, c, :]))
+            for path in range(PATHS):
+                for c in range(PATH_PASSES):
+                    rows = path_w[path, c * K_PASS : (c + 1) * K_PASS, :].rearrange("(t p) n -> p t n", p=P)
+                    chunks.append((rows, PATH_VECTOR_COLS, w2_codes[:, path, c, :], w2_scales[:, path, c, :]))
+            grouped = {}
+
+            def regroup_chunk(i):
+                grouped[i] = load_and_regroup(chunks[i][0], chunks[i][1])
+
+            def quantise_chunk(i):
+                quantise_weight(grouped[i], chunks[i][2], chunks[i][3])
+
+            for tt in range(TOKEN_TILES):
+                e_words = e_raw[tt][:].bitcast(F32)
+                e_grouped = stage.tile([P, K_ENT], BF16, tag="grouped", align_bytes=64)
+                grouped_words = e_grouped[:].bitcast(F32).rearrange("p (c r u) -> p c r u", c=ENT_PASSES, u=2)
+                for pair in range(ENT_PASSES // 2):
+                    bank = psum.tile([P, 2, 2, P], F32, tag="bank")
+                    for c2 in range(2):
+                        for u in range(2):
+                            first = (2 * pair + c2) * 2 * P + u * P
+                            nc.tensor.transpose(bank[:, c2, u, :], e_words[:, first : first + P], ident_f32[:])
+                    planes = bank[:].rearrange("p c u r -> p c r u")
+                    if pair < 3:
+                        nc.scalar.copy(out=grouped_words[:, 2 * pair : 2 * pair + 2], in_=planes)
+                    else:
+                        nc.vector.tensor_copy(out=grouped_words[:, 2 * pair : 2 * pair + 2], in_=planes)
+                nc.vector.quantize_mx(
+                    out=e_codes[:, tt].rearrange("p c r -> p (c r)").bitcast(FP8X4),
+                    scales=e_scales[:, tt].rearrange("p c r -> p (c r)"),
+                    in_=e_grouped[:],
+                )
+
+            ent_acc = [
+                [psum.tile([P, BANK], F32, tag="bank", name="ent_acc_%d_%d" % (tt, half)) for half in range(HALVES)]
+                for tt in range(TOKEN_TILES)
+            ]
+            for i in range(ENT_PASSES + 1):
+                regroup_chunk(i)
+                if i == 0:
+                    continue
+                c = i - 1
+                quantise_chunk(c)
+                for tt in range(TOKEN_TILES):
+                    for half in range(HALVES):
+                        cols = slice(half * BANK, (half + 1) * BANK)
+                        nc.tensor.matmul_mx(
+                            out=ent_acc[tt][half][:],
+                            lhsT=e_codes[:, tt, c, :].bitcast(FP8X4),
+                            lhsT_scale=e_scales[:, tt, c, :],
+                            rhs=w1_codes[:, c, cols].bitcast(FP8X4),
+                            rhs_scale=w1_scales[:, c, cols],
+                            start=(c == 0),
+                            stop=(c == ENT_PASSES - 1),
+                        )
+
+        tail = ctx.enter_context(tc.tile_pool(name="tail", bufs=1))
+        interf_t = tail.tile([P, FEATURE_TILES, TOKENS], F32)
+        neg_mean, std = {}, {}
+
+        def first_norm_stats(tt):
+            neg_mean[tt] = add_and_mean(x_all[:, tt, :], ent_acc[tt], x_all[:, tt, :])
+            std[tt] = deviation(x_all[:, tt, :], neg_mean[tt])
+
+        def first_norm_apply(tt):
+            centre_and_gain(hn_all[:, tt, :], x_all[:, tt, :], neg_mean[tt], ln3_g_spread[:])
+            divide_and_shift(hn_all[:, tt, :], std[tt], ln3_b_spread[:])
+
+        def transpose_hn(tt):
+            tokens = slice(tt * P, (tt + 1) * P)
+            for c in range(PATH_PASSES):
+                bank = psum.tile([P, PACK, P], F32, tag="bank")
+                for t in range(PACK):
+                    first = c * K_PASS + t * P
+                    nc.tensor.transpose(bank[:, t, :], hn_all[:, tt, first : first + P], ident_f32[:])
+                nc.scalar.copy(out=hn_grouped[:, c, tokens, :], in_=bank[:].rearrange("p t r -> p r t"))
+
+        def quantise_hn(tt):
+            tokens = slice(tt * P, (tt + 1) * P)
+            for c in range(PATH_PASSES):
+                nc.vector.quantize_mx(
+                    out=hn_codes[:, c, tokens].bitcast(FP8X4),
+                    scales=hn_scales[:, c, tokens],
+                    in_=hn_grouped[:, c, tokens, :].rearrange("p r t -> p (r t)"),
+                )
+
+        def stage2(group):
+            group_tokens = slice(group * GROUP, (group + 1) * GROUP)
+            for j in range(FEATURE_TILES):
+                feats = slice(j * P, (j + 1) * P)
+                bank = psum.tile([P, PATHS, GROUP], F32, tag="bank")
+                for path in range(PATHS):
+                    for c in range(PATH_PASSES):
+                        nc.tensor.matmul_mx(
+                            out=bank[:, path, :],
+                            lhsT=w2_codes[:, path, c, feats].bitcast(FP8X4),
+                            lhsT_scale=w2_scales[:, path, c, feats],
+                            rhs=hn_codes[:, c, group_tokens].bitcast(FP8X4),
+                            rhs_scale=hn_scales[:, c, group_tokens],
+                            start=(c == 0),
+                            stop=(c == PATH_PASSES - 1),
+                        )
+                nc.scalar.activation(
+                    out=interf_t[:, j, group_tokens], in_=bank[:, 0, :], func=ACT.Identity,
+                    scale=mod[:, 0, j : j + 1], bias=bias_sum[:, j : j + 1],
+                )
+                nc.vector.scalar_tensor_tensor(
+                    out=interf_t[:, j, group_tokens], in0=bank[:, 1, :], scalar=mod[:, 1, j : j + 1],
+                    in1=interf_t[:, j, group_tokens], op0=ALU.mult, op1=ALU.add,
+                )
+
+        def second_norm_stats(tt):
+            tokens = slice(tt * P, (tt + 1) * P)
+            banks = []
+            for half in range(HALVES):
+                bank = psum.tile([P, BANK], F32, tag="bank")
+                for q in range(BANK // P):
+                    j = half * (BANK // P) + q
+                    nc.tensor.transpose(bank[:, q * P : (q + 1) * P], interf_t[:, j, tokens], ident_f32[:])
+                banks.append(bank)
+            neg_mean[tt] = add_and_mean(x_all[:, tt, :], banks, hn_all[:, tt, :])
+            std[tt] = deviation(x_all[:, tt, :], neg_mean[tt])
+
+        def second_norm_apply(tt):
+            centre_and_gain(hn_all[:, tt, :], x_all[:, tt, :], neg_mean[tt], ln4_g_spread[:])
+            divide_and_shift(hn_all[:, tt, :], std[tt], ln4_b_spread[:])
+            nc.sync.dma_start(out=out_rows[tt * P : (tt + 1) * P, :], in_=hn_all[:, tt, :])
+
+        regroup_chunk(9)
+        quantise_chunk(8)
+        first_norm_stats(0)
+        first_norm_stats(1)
+        regroup_chunk(10)
+        quantise_chunk(9)
+        first_norm_apply(0)
+        first_norm_apply(1)
+        transpose_hn(0)
+        transpose_hn(1)
+        regroup_chunk(11)
+        quantise_chunk(10)
+        ln4_g_spread = consts.tile([P, FEATURES], BF16)
+        nc.sync.dma_start(out=ln4_g_spread[:], in_=ln4_g.partition_broadcast(P))
+        ln4_b_spread = consts.tile([P, FEATURES], BF16)
+        nc.sync.dma_start(out=ln4_b_spread[:], in_=ln4_b.partition_broadcast(P))
+        first_norm_stats(2)
+        first_norm_stats(3)
+        quantise_chunk(11)
+        quantise_hn(0)
+        quantise_hn(1)
+        first_norm_apply(2)
+        first_norm_apply(3)
+        stage2(0)
+        transpose_hn(2)
+        transpose_hn(3)
+        second_norm_stats(0)
+        second_norm_stats(1)
+        quantise_hn(2)
+        quantise_hn(3)
+        second_norm_apply(0)
+        second_norm_apply(1)
+        stage2(1)
+        second_norm_stats(2)
+        second_norm_stats(3)
+        second_norm_apply(2)
+        second_norm_apply(3)

@@ -133,14 +133,23 @@ def tile_quantuminspiredneuralcore_pb_kernel(
 
         h_sb = keep.tile([P, TOKEN_TILES, FEATURES], BF16)
         e_raw = [stage.tile([P, K_ENT], BF16, tag="raw", name="e_raw_%d" % tt) for tt in range(TOKEN_TILES)]
-        nc.scalar.dma_start(out=early_rows[0:1, :], in_=ent_pb.unsqueeze(0))
-        nc.scalar.dma_start(out=vec_rows[0:1, :], in_=ln3_g.unsqueeze(0))
-        nc.scalar.dma_start(out=vec_rows[1:2, :], in_=ln3_b.unsqueeze(0))
-        nc.scalar.dma_start(out=vec_rows[2:4, :], in_=path_b)
-        nc.scalar.dma_start(out=vec_rows[4:6, :], in_=phase)
+        def load_e(tt, half):
+            cols = slice(half * (K_ENT // 2), (half + 1) * (K_ENT // 2))
+            nc.sync.dma_start(out=e_raw[tt][:, cols], in_=e_rows[tt * P : (tt + 1) * P, cols])
+
+        load_e(0, 0)
+        nc.sync.dma_start(out=early_rows[0:1, :], in_=ent_pb.unsqueeze(0))
+        nc.sync.dma_start(out=vec_rows[0:1, :], in_=ln3_g.unsqueeze(0))
+        nc.sync.dma_start(out=vec_rows[1:2, :], in_=ln3_b.unsqueeze(0))
+        nc.sync.dma_start(out=vec_rows[2:4, :], in_=path_b)
+        nc.sync.dma_start(out=vec_rows[4:6, :], in_=phase)
+        load_e(0, 1)
+        load_e(1, 0)
+        load_e(1, 1)
         nc.sync.dma_start(out=h_sb[:], in_=h_rows.rearrange("(t p) f -> p t f", p=P))
-        for tt in range(TOKEN_TILES):
-            nc.sync.dma_start(out=e_raw[tt][:], in_=e_rows[tt * P : (tt + 1) * P, :])
+        for tt in range(2, TOKEN_TILES):
+            load_e(tt, 0)
+            load_e(tt, 1)
         table_warm = consts.tile([P, 1], F32)
         nc.scalar.activation(out=table_warm[:], in_=eps[:], func=ACT.Sin)
 
@@ -183,7 +192,7 @@ def tile_quantuminspiredneuralcore_pb_kernel(
         nc.scalar.activation(out=sin_half[:], in_=angle[:], func=ACT.Sin, scale=0.5)
 
         for tt in range(TOKEN_TILES):
-            nc.vector.tensor_tensor(out=x_all[:, tt, :], in0=h_sb[:, tt, :], in1=ent_pb_spread[:], op=ALU.add)
+            nc.gpsimd.tensor_tensor(out=x_all[:, tt, :], in0=h_sb[:, tt, :], in1=ent_pb_spread[:], op=ALU.add)
 
         mod = consts.tile([P, PATHS, FEATURE_TILES], F32)
         nc.vector.tensor_tensor(out=mod[:], in0=sin_half[:], in1=sin_half[:], op=ALU.mult)
@@ -260,7 +269,7 @@ def tile_quantuminspiredneuralcore_pb_kernel(
                         )
 
         tail = ctx.enter_context(tc.tile_pool(name="tail", bufs=1))
-        interf_t = tail.tile([P, FEATURE_TILES, TOKENS], F32)
+        interf_t = tail.tile([P, PATHS, FEATURE_TILES, TOKENS], F32)
         neg_mean, std = {}, {}
 
         def first_norm_stats(tt):
@@ -306,12 +315,12 @@ def tile_quantuminspiredneuralcore_pb_kernel(
                             stop=(c == PATH_PASSES - 1),
                         )
                 nc.scalar.activation(
-                    out=interf_t[:, j, group_tokens], in_=bank[:, 0, :], func=ACT.Identity,
+                    out=interf_t[:, 0, j, group_tokens], in_=bank[:, 0, :], func=ACT.Identity,
                     scale=mod[:, 0, j : j + 1], bias=bias_sum[:, j : j + 1],
                 )
-                nc.vector.scalar_tensor_tensor(
-                    out=interf_t[:, j, group_tokens], in0=bank[:, 1, :], scalar=mod[:, 1, j : j + 1],
-                    in1=interf_t[:, j, group_tokens], op0=ALU.mult, op1=ALU.add,
+                nc.scalar.activation(
+                    out=interf_t[:, 1, j, group_tokens], in_=bank[:, 1, :], func=ACT.Identity,
+                    scale=mod[:, 1, j : j + 1],
                 )
 
         def second_norm_stats(tt):
@@ -321,7 +330,11 @@ def tile_quantuminspiredneuralcore_pb_kernel(
                 bank = psum.tile([P, BANK], F32, tag="bank")
                 for q in range(BANK // P):
                     j = half * (BANK // P) + q
-                    nc.tensor.transpose(bank[:, q * P : (q + 1) * P], interf_t[:, j, tokens], ident_f32[:])
+                    for path in range(PATHS):
+                        nc.tensor.matmul(
+                            out=bank[:, q * P : (q + 1) * P], lhsT=interf_t[:, path, j, tokens], rhs=ident_f32[:],
+                            is_transpose=True, start=(path == 0), stop=(path == PATHS - 1),
+                        )
                 banks.append(bank)
             neg_mean[tt] = add_and_mean(x_all[:, tt, :], banks, hn_all[:, tt, :])
             std[tt] = deviation(x_all[:, tt, :], neg_mean[tt])

@@ -17,6 +17,7 @@ P = 128
 PACK = 4
 K_PASS = P * PACK
 BANK = 512
+PSUM_BANKS = 8
 
 TOKENS = 512
 TOKEN_TILES = TOKENS // P
@@ -27,12 +28,11 @@ K_ENT = 4096
 ENT_PASSES = K_ENT // K_PASS
 PATHS = 2
 PATH_PASSES = FEATURES // K_PASS
-GROUP_TILES = 2
-GROUP = GROUP_TILES * P
 EPS = 1e-5
 
-ENT_VECTOR_COLS = 512
-PATH_VECTOR_COLS = 256
+VECTOR_COLS = FEATURES // 2
+
+TILE_SKEW = 2
 
 TWO_PI_HEAD = 6.28125
 TWO_PI_REST = 2.0 * math.pi - TWO_PI_HEAD
@@ -55,90 +55,30 @@ def tile_quantuminspiredneuralcore_pb_kernel(
         keep = ctx.enter_context(tc.tile_pool(name="keep", bufs=1))
         stats = ctx.enter_context(tc.tile_pool(name="stats", bufs=TOKEN_TILES))
         scratch = ctx.enter_context(tc.tile_pool(name="scratch", bufs=2))
-        stage = ctx.enter_context(tc.tile_pool(name="stage", bufs=4))
-        psum = ctx.enter_context(tc.psum_pool(name="psum", bufs=8))
-
-        def zeroed_rows(name):
-            rows = consts.tile([P, FEATURES], BF16, name=name)
-            nc.vector.memset(rows[:].bitcast(I32), 0)
-            return rows
-
-        def spread_row(rows, r, name):
-            pick_row = ident_bf16[:, r : r + 1].to_broadcast([P, P])
-            bank = psum.tile([P, FEATURES], BF16, tag="bank")
-            for half in range(HALVES):
-                cols = slice(half * BANK, (half + 1) * BANK)
-                nc.tensor.matmul(out=bank[:, cols], lhsT=pick_row, rhs=rows[:, cols], start=True, stop=True)
-            spread = consts.tile([P, FEATURES], BF16, name=name)
-            nc.scalar.copy(out=spread[:], in_=bank[:])
-            return spread
-
-        def load_and_regroup(rows_by_slot, vector_cols):
-            raw = stage.tile([P, PACK * FEATURES], BF16, tag="raw")
-            nc.sync.dma_start(out=raw[:].rearrange("p (a b) -> p a b", a=rows_by_slot.shape[1]), in_=rows_by_slot)
-            grouped = stage.tile([P, FEATURES, PACK], BF16, tag="grouped", align_bytes=64)
-            src = raw[:].rearrange("p (t c i) -> p c t i", t=PACK, i=4)
-            dst = grouped[:].rearrange("p (c i) t -> p c t i", i=4)
-            split = vector_cols // 4
-            nc.vector.tensor_copy(out=dst[:, :split], in_=src[:, :split])
-            nc.scalar.copy(out=dst[:, split:], in_=src[:, split:])
-            return grouped
-
-        def quantise_weight(grouped, codes, scales):
-            nc.vector.quantize_mx(
-                out=codes.bitcast(FP8X4), scales=scales, in_=grouped[:].rearrange("p n t -> p (n t)")
-            )
-
-        def add_and_mean(dst, banks, addend):
-            sums = stats.tile([P, HALVES], F32)
-            for half in range(HALVES):
-                cols = slice(half * BANK, (half + 1) * BANK)
-                nc.vector.scalar_tensor_tensor(
-                    out=dst[:, cols], in0=banks[half][:], scalar=0.0, in1=addend[:, cols],
-                    op0=ALU.add, op1=ALU.add, accum_out=sums[:, half : half + 1],
-                )
-            neg_mean = stats.tile([P, 1], F32)
-            nc.vector.tensor_scalar(
-                out=neg_mean[:], in0=sums[:, 0:1], scalar1=sums[:, 1:2], scalar2=-1.0 / FEATURES,
-                op0=ALU.add, op1=ALU.mult,
-            )
-            return neg_mean
-
-        def deviation(src, neg_mean):
-            squares = scratch.tile([P, FEATURES], BF16)
-            sum_sq = stats.tile([P, 1], F32)
-            nc.scalar.activation(
-                out=squares[:], in_=src, func=ACT.Square, bias=neg_mean[:], scale=1.0, accum_out=sum_sq[:]
-            )
-            std = stats.tile([P, 1], F32)
-            nc.scalar.activation(out=std[:], in_=sum_sq[:], func=ACT.Sqrt, bias=eps[:], scale=1.0 / FEATURES)
-            return std
-
-        def centre_and_gain(dst, src, neg_mean, gain):
-            nc.vector.scalar_tensor_tensor(out=dst, in0=src, scalar=neg_mean[:], in1=gain, op0=ALU.add, op1=ALU.mult)
-
-        def divide_and_shift(dst, std, shift):
-            rstd = stats.tile([P, 1], F32)
-            nc.vector.reciprocal(out=rstd[:], in_=std[:])
-            nc.vector.scalar_tensor_tensor(out=dst, in0=dst, scalar=rstd[:], in1=shift, op0=ALU.mult, op1=ALU.add)
+        raw_pool = ctx.enter_context(tc.tile_pool(name="raw", bufs=5))
+        grouped_pool = ctx.enter_context(tc.tile_pool(name="grouped", bufs=3))
+        psum = ctx.enter_context(tc.psum_pool(name="psum", bufs=PSUM_BANKS))
 
         ident_f32 = consts.tile([P, P], F32)
         make_identity(nc, ident_f32[:])
-        early_rows = zeroed_rows("early_rows")
-        vec_rows = zeroed_rows("vec_rows")
         eps = consts.tile([P, 1], F32)
         nc.vector.memset(eps[:], EPS)
+        ent_pb_rows = consts.tile([P, FEATURES], BF16)
+        nc.vector.memset(ent_pb_rows[:].bitcast(I32), 0)
+        vec_rows = consts.tile([P, FEATURES], BF16)
+        nc.vector.memset(vec_rows[:].bitcast(I32), 0)
         ident_bf16 = consts.tile([P, P], BF16)
         nc.vector.tensor_copy(out=ident_bf16[:], in_=ident_f32[:])
 
         h_sb = keep.tile([P, TOKEN_TILES, FEATURES], BF16)
-        e_raw = [stage.tile([P, K_ENT], BF16, tag="raw", name="e_raw_%d" % tt) for tt in range(TOKEN_TILES)]
+        e_raw = [raw_pool.tile([P, K_ENT], BF16, tag="raw", name="e_raw_%d" % tt) for tt in range(TOKEN_TILES)]
+
         def load_e(tt, half):
             cols = slice(half * (K_ENT // 2), (half + 1) * (K_ENT // 2))
             nc.sync.dma_start(out=e_raw[tt][:, cols], in_=e_rows[tt * P : (tt + 1) * P, cols])
 
         load_e(0, 0)
-        nc.sync.dma_start(out=early_rows[0:1, :], in_=ent_pb.unsqueeze(0))
+        nc.sync.dma_start(out=ent_pb_rows[0:1, :], in_=ent_pb.unsqueeze(0))
         nc.sync.dma_start(out=vec_rows[0:1, :], in_=ln3_g.unsqueeze(0))
         nc.sync.dma_start(out=vec_rows[1:2, :], in_=ln3_b.unsqueeze(0))
         nc.sync.dma_start(out=vec_rows[2:4, :], in_=path_b)
@@ -153,15 +93,17 @@ def tile_quantuminspiredneuralcore_pb_kernel(
         table_warm = consts.tile([P, 1], F32)
         nc.scalar.activation(out=table_warm[:], in_=eps[:], func=ACT.Sin)
 
-        x_all = keep.tile([P, TOKEN_TILES, FEATURES], F32)
-        hn_all = keep.tile([P, TOKEN_TILES, FEATURES], F32)
-        hn_grouped = keep.tile([P, PATH_PASSES, TOKENS, PACK], BF16, align_bytes=64)
-        hn_codes = keep.tile([P, PATH_PASSES, TOKENS], U32, align_bytes=64)
-        hn_scales = keep.tile([P, PATH_PASSES, TOKENS], U8, align_bytes=64)
-        w2_codes = keep.tile([P, PATHS, PATH_PASSES, FEATURES], U32, align_bytes=64)
-        w2_scales = keep.tile([P, PATHS, PATH_PASSES, FEATURES], U8, align_bytes=64)
+        def spread_row(rows, r, name):
+            pick_row = ident_bf16[:, r : r + 1].to_broadcast([P, P])
+            bank = psum.tile([P, FEATURES], BF16, tag="bank")
+            for half in range(HALVES):
+                cols = slice(half * BANK, (half + 1) * BANK)
+                nc.tensor.matmul(out=bank[:, cols], lhsT=pick_row, rhs=rows[:, cols], start=True, stop=True)
+            spread = consts.tile([P, FEATURES], BF16, name=name)
+            nc.scalar.copy(out=spread[:], in_=bank[:])
+            return spread
 
-        ent_pb_spread = spread_row(early_rows, 0, "ent_pb_spread")
+        ent_pb_spread = spread_row(ent_pb_rows, 0, "ent_pb_spread")
         ln3_g_spread = spread_row(vec_rows, 0, "ln3_g_spread")
         ln3_b_spread = spread_row(vec_rows, 1, "ln3_b_spread")
 
@@ -190,10 +132,6 @@ def tile_quantuminspiredneuralcore_pb_kernel(
         nc.scalar.activation(out=sin_full[:], in_=angle[:], func=ACT.Sin)
         sin_half = consts.tile([P, PATHS, FEATURE_TILES], F32)
         nc.scalar.activation(out=sin_half[:], in_=angle[:], func=ACT.Sin, scale=0.5)
-
-        for tt in range(TOKEN_TILES):
-            nc.gpsimd.tensor_tensor(out=x_all[:, tt, :], in0=h_sb[:, tt, :], in1=ent_pb_spread[:], op=ALU.add)
-
         mod = consts.tile([P, PATHS, FEATURE_TILES], F32)
         nc.vector.tensor_tensor(out=mod[:], in0=sin_half[:], in1=sin_half[:], op=ALU.mult)
         nc.vector.tensor_scalar(out=mod[:], in0=mod[:], scalar1=-2.0, scalar2=1.0, op0=ALU.mult, op1=ALU.add)
@@ -203,30 +141,28 @@ def tile_quantuminspiredneuralcore_pb_kernel(
         bias_sum = consts.tile([P, FEATURE_TILES], F32)
         nc.vector.tensor_tensor(out=bias_sum[:], in0=bias_mod[:, 0, :], in1=bias_mod[:, 1, :], op=ALU.add)
 
+        x_all = keep.tile([P, TOKEN_TILES, FEATURES], F32)
+        for tt in range(TOKEN_TILES):
+            nc.gpsimd.tensor_tensor(out=x_all[:, tt, :], in0=h_sb[:, tt, :], in1=ent_pb_spread[:], op=ALU.add)
+
+        hn_all = keep.tile([P, TOKEN_TILES, FEATURES], F32)
+        hn_grouped = keep.tile([P, TOKEN_TILES, PATH_PASSES, P, PACK], BF16, align_bytes=64)
+        hn_codes = keep.tile([P, TOKEN_TILES, PATH_PASSES, P], U32, align_bytes=64)
+        hn_scales = keep.tile([P, TOKEN_TILES, PATH_PASSES, P], U8, align_bytes=64)
+        w2_codes = keep.tile([P, PATHS, PATH_PASSES, FEATURES], U32, align_bytes=64)
+        w2_scales = keep.tile([P, PATHS, PATH_PASSES, FEATURES], U8, align_bytes=64)
+        ln4_g_spread = consts.tile([P, FEATURES], BF16)
+        ln4_b_spread = consts.tile([P, FEATURES], BF16)
+
         with tc.tile_pool(name="stage1", bufs=1) as stage1:
             e_codes = stage1.tile([P, TOKEN_TILES, ENT_PASSES, P], U32, align_bytes=64)
             e_scales = stage1.tile([P, TOKEN_TILES, ENT_PASSES, P], U8, align_bytes=64)
             w1_codes = stage1.tile([P, ENT_PASSES, FEATURES], U32, align_bytes=64)
             w1_scales = stage1.tile([P, ENT_PASSES, FEATURES], U8, align_bytes=64)
-            chunks = []
-            for c in range(ENT_PASSES):
-                rows = ent_pw[c * K_PASS : (c + 1) * K_PASS, :].rearrange("(u p s) n -> p u (s n)", u=2, s=2)
-                chunks.append((rows, ENT_VECTOR_COLS, w1_codes[:, c, :], w1_scales[:, c, :]))
-            for path in range(PATHS):
-                for c in range(PATH_PASSES):
-                    rows = path_w[path, c * K_PASS : (c + 1) * K_PASS, :].rearrange("(t p) n -> p t n", p=P)
-                    chunks.append((rows, PATH_VECTOR_COLS, w2_codes[:, path, c, :], w2_scales[:, path, c, :]))
-            grouped = {}
-
-            def regroup_chunk(i):
-                grouped[i] = load_and_regroup(chunks[i][0], chunks[i][1])
-
-            def quantise_chunk(i):
-                quantise_weight(grouped[i], chunks[i][2], chunks[i][3])
 
             for tt in range(TOKEN_TILES):
                 e_words = e_raw[tt][:].bitcast(F32)
-                e_grouped = stage.tile([P, K_ENT], BF16, tag="grouped", align_bytes=64)
+                e_grouped = grouped_pool.tile([P, K_ENT], BF16, tag="grouped", align_bytes=64)
                 grouped_words = e_grouped[:].bitcast(F32).rearrange("p (c r u) -> p c r u", c=ENT_PASSES, u=2)
                 for pair in range(ENT_PASSES // 2):
                     bank = psum.tile([P, 2, 2, P], F32, tag="bank")
@@ -245,16 +181,42 @@ def tile_quantuminspiredneuralcore_pb_kernel(
                     in_=e_grouped[:],
                 )
 
+            chunks = []
+            for c in range(ENT_PASSES):
+                rows = ent_pw[c * K_PASS : (c + 1) * K_PASS, :].rearrange("(u p s) n -> p u (s n)", u=2, s=2)
+                chunks.append((rows, w1_codes[:, c, :], w1_scales[:, c, :]))
+            for path in range(PATHS):
+                for c in range(PATH_PASSES):
+                    rows = path_w[path, c * K_PASS : (c + 1) * K_PASS, :].rearrange("(t p) n -> p t n", p=P)
+                    chunks.append((rows, w2_codes[:, path, c, :], w2_scales[:, path, c, :]))
+            grouped = {}
             ent_acc = [
                 [psum.tile([P, BANK], F32, tag="bank", name="ent_acc_%d_%d" % (tt, half)) for half in range(HALVES)]
                 for tt in range(TOKEN_TILES)
             ]
-            for i in range(ENT_PASSES + 1):
-                regroup_chunk(i)
+
+            def weight_step(i):
+                if i < len(chunks):
+                    rows = chunks[i][0]
+                    raw = raw_pool.tile([P, PACK * FEATURES], BF16, tag="raw")
+                    nc.sync.dma_start(out=raw[:].rearrange("p (a b) -> p a b", a=rows.shape[1]), in_=rows)
+                    grouped[i] = grouped_pool.tile([P, FEATURES, PACK], BF16, tag="grouped", name="w_grouped", align_bytes=64)
+                    src = raw[:].rearrange("p (t c i) -> p c t i", t=PACK, i=4)
+                    dst = grouped[i][:].rearrange("p (c i) t -> p c t i", i=4)
+                    split = VECTOR_COLS // 4
+                    nc.vector.tensor_copy(out=dst[:, :split], in_=src[:, :split])
+                    nc.scalar.copy(out=dst[:, split:], in_=src[:, split:])
+                if i == len(chunks) - 1:
+                    nc.sync.dma_start(out=ln4_g_spread[:], in_=ln4_g.partition_broadcast(P))
+                    nc.sync.dma_start(out=ln4_b_spread[:], in_=ln4_b.partition_broadcast(P))
                 if i == 0:
-                    continue
+                    return
                 c = i - 1
-                quantise_chunk(c)
+                nc.vector.quantize_mx(
+                    out=chunks[c][1].bitcast(FP8X4), scales=chunks[c][2], in_=grouped[c][:].rearrange("p n t -> p (n t)")
+                )
+                if c >= ENT_PASSES:
+                    return
                 for tt in range(TOKEN_TILES):
                     for half in range(HALVES):
                         cols = slice(half * BANK, (half + 1) * BANK)
@@ -268,64 +230,107 @@ def tile_quantuminspiredneuralcore_pb_kernel(
                             stop=(c == ENT_PASSES - 1),
                         )
 
+            for i in range(ENT_PASSES + 1):
+                weight_step(i)
+
         tail = ctx.enter_context(tc.tile_pool(name="tail", bufs=1))
         interf_t = tail.tile([P, PATHS, FEATURE_TILES, TOKENS], F32)
-        neg_mean, std = {}, {}
 
-        def first_norm_stats(tt):
-            neg_mean[tt] = add_and_mean(x_all[:, tt, :], ent_acc[tt], x_all[:, tt, :])
-            std[tt] = deviation(x_all[:, tt, :], neg_mean[tt])
+        row_sums, neg_mean, rstd, hn_banks, y_banks = {}, {}, {}, {}, {}
 
-        def first_norm_apply(tt):
-            centre_and_gain(hn_all[:, tt, :], x_all[:, tt, :], neg_mean[tt], ln3_g_spread[:])
-            divide_and_shift(hn_all[:, tt, :], std[tt], ln3_b_spread[:])
+        def add_and_sum(tt, dst, banks, addend):
+            row_sums[tt] = stats.tile([P, HALVES], F32, name="row_sums")
+            for half in range(HALVES):
+                cols = slice(half * BANK, (half + 1) * BANK)
+                nc.vector.scalar_tensor_tensor(
+                    out=dst[:, cols], in0=banks[half][:], scalar=0.0, in1=addend[:, cols],
+                    op0=ALU.add, op1=ALU.add, accum_out=row_sums[tt][:, half : half + 1],
+                )
+
+        def statistics(tt, src):
+            scaled_sums = stats.tile([P, HALVES], F32)
+            neg_mean[tt] = stats.tile([P, 1], F32, name="neg_mean")
+            nc.scalar.activation(
+                out=scaled_sums[:], in_=row_sums[tt][:], func=ACT.Identity, scale=-1.0 / FEATURES,
+                accum_out=neg_mean[tt][:],
+            )
+            squares = scratch.tile([P, FEATURES], BF16)
+            sum_sq = stats.tile([P, 1], F32)
+            nc.scalar.activation(
+                out=squares[:], in_=src, func=ACT.Square, bias=neg_mean[tt][:], scale=1.0, accum_out=sum_sq[:]
+            )
+            rstd[tt] = stats.tile([P, 1], F32, name="rstd")
+            nc.scalar.activation(
+                out=rstd[tt][:], in_=sum_sq[:], func=ACT.Abs_reciprocal_sqrt, bias=eps[:], scale=1.0 / FEATURES
+            )
+
+        def centre_and_gain(tt, dst, src, gain):
+            nc.vector.scalar_tensor_tensor(
+                out=dst, in0=src, scalar=neg_mean[tt][:], in1=gain[:], op0=ALU.add, op1=ALU.mult
+            )
+
+        def scale_and_shift(tt, dst, shift):
+            nc.vector.scalar_tensor_tensor(
+                out=dst, in0=dst, scalar=rstd[tt][:], in1=shift[:], op0=ALU.mult, op1=ALU.add
+            )
+
+        def add_ent(tt):
+            add_and_sum(tt, x_all[:, tt, :], ent_acc[tt], x_all[:, tt, :])
+
+        def first_norm_centre(tt):
+            statistics(tt, x_all[:, tt, :])
+            centre_and_gain(tt, hn_all[:, tt, :], x_all[:, tt, :], ln3_g_spread)
+
+        def first_norm_scale(tt):
+            scale_and_shift(tt, hn_all[:, tt, :], ln3_b_spread)
 
         def transpose_hn(tt):
-            tokens = slice(tt * P, (tt + 1) * P)
+            hn_banks[tt] = []
             for c in range(PATH_PASSES):
                 bank = psum.tile([P, PACK, P], F32, tag="bank")
                 for t in range(PACK):
                     first = c * K_PASS + t * P
                     nc.tensor.transpose(bank[:, t, :], hn_all[:, tt, first : first + P], ident_f32[:])
-                nc.scalar.copy(out=hn_grouped[:, c, tokens, :], in_=bank[:].rearrange("p t r -> p r t"))
+                hn_banks[tt].append(bank)
+
+        def round_hn(tt):
+            for c in range(PATH_PASSES):
+                nc.scalar.copy(out=hn_grouped[:, tt, c], in_=hn_banks[tt][c][:].rearrange("p t r -> p r t"))
 
         def quantise_hn(tt):
-            tokens = slice(tt * P, (tt + 1) * P)
-            for c in range(PATH_PASSES):
-                nc.vector.quantize_mx(
-                    out=hn_codes[:, c, tokens].bitcast(FP8X4),
-                    scales=hn_scales[:, c, tokens],
-                    in_=hn_grouped[:, c, tokens, :].rearrange("p r t -> p (r t)"),
-                )
+            nc.vector.quantize_mx(
+                out=hn_codes[:, tt].rearrange("p c r -> p (c r)").bitcast(FP8X4),
+                scales=hn_scales[:, tt].rearrange("p c r -> p (c r)"),
+                in_=hn_grouped[:, tt].rearrange("p c r t -> p (c r t)"),
+            )
 
-        def stage2(group):
-            group_tokens = slice(group * GROUP, (group + 1) * GROUP)
+        def stage2(tt):
+            tokens = slice(tt * P, (tt + 1) * P)
             for j in range(FEATURE_TILES):
                 feats = slice(j * P, (j + 1) * P)
-                bank = psum.tile([P, PATHS, GROUP], F32, tag="bank")
+                bank = psum.tile([P, PATHS, P], F32, tag="bank")
                 for path in range(PATHS):
                     for c in range(PATH_PASSES):
                         nc.tensor.matmul_mx(
                             out=bank[:, path, :],
                             lhsT=w2_codes[:, path, c, feats].bitcast(FP8X4),
                             lhsT_scale=w2_scales[:, path, c, feats],
-                            rhs=hn_codes[:, c, group_tokens].bitcast(FP8X4),
-                            rhs_scale=hn_scales[:, c, group_tokens],
+                            rhs=hn_codes[:, tt, c, :].bitcast(FP8X4),
+                            rhs_scale=hn_scales[:, tt, c, :],
                             start=(c == 0),
                             stop=(c == PATH_PASSES - 1),
                         )
                 nc.scalar.activation(
-                    out=interf_t[:, 0, j, group_tokens], in_=bank[:, 0, :], func=ACT.Identity,
+                    out=interf_t[:, 0, j, tokens], in_=bank[:, 0, :], func=ACT.Identity,
                     scale=mod[:, 0, j : j + 1], bias=bias_sum[:, j : j + 1],
                 )
                 nc.scalar.activation(
-                    out=interf_t[:, 1, j, group_tokens], in_=bank[:, 1, :], func=ACT.Identity,
-                    scale=mod[:, 1, j : j + 1],
+                    out=interf_t[:, 1, j, tokens], in_=bank[:, 1, :], func=ACT.Identity, scale=mod[:, 1, j : j + 1]
                 )
 
-        def second_norm_stats(tt):
+        def transpose_interf(tt):
             tokens = slice(tt * P, (tt + 1) * P)
-            banks = []
+            y_banks[tt] = []
             for half in range(HALVES):
                 bank = psum.tile([P, BANK], F32, tag="bank")
                 for q in range(BANK // P):
@@ -335,49 +340,27 @@ def tile_quantuminspiredneuralcore_pb_kernel(
                             out=bank[:, q * P : (q + 1) * P], lhsT=interf_t[:, path, j, tokens], rhs=ident_f32[:],
                             is_transpose=True, start=(path == 0), stop=(path == PATHS - 1),
                         )
-                banks.append(bank)
-            neg_mean[tt] = add_and_mean(x_all[:, tt, :], banks, hn_all[:, tt, :])
-            std[tt] = deviation(x_all[:, tt, :], neg_mean[tt])
+                y_banks[tt].append(bank)
 
-        def second_norm_apply(tt):
-            centre_and_gain(hn_all[:, tt, :], x_all[:, tt, :], neg_mean[tt], ln4_g_spread[:])
-            divide_and_shift(hn_all[:, tt, :], std[tt], ln4_b_spread[:])
+        def add_hn(tt):
+            add_and_sum(tt, x_all[:, tt, :], y_banks[tt], hn_all[:, tt, :])
+
+        def second_norm_centre(tt):
+            statistics(tt, x_all[:, tt, :])
+            centre_and_gain(tt, hn_all[:, tt, :], x_all[:, tt, :], ln4_g_spread)
+
+        def second_norm_scale(tt):
+            scale_and_shift(tt, hn_all[:, tt, :], ln4_b_spread)
             nc.sync.dma_start(out=out_rows[tt * P : (tt + 1) * P, :], in_=hn_all[:, tt, :])
 
-        regroup_chunk(9)
-        quantise_chunk(8)
-        first_norm_stats(0)
-        first_norm_stats(1)
-        regroup_chunk(10)
-        quantise_chunk(9)
-        first_norm_apply(0)
-        first_norm_apply(1)
-        transpose_hn(0)
-        transpose_hn(1)
-        regroup_chunk(11)
-        quantise_chunk(10)
-        ln4_g_spread = consts.tile([P, FEATURES], BF16)
-        nc.sync.dma_start(out=ln4_g_spread[:], in_=ln4_g.partition_broadcast(P))
-        ln4_b_spread = consts.tile([P, FEATURES], BF16)
-        nc.sync.dma_start(out=ln4_b_spread[:], in_=ln4_b.partition_broadcast(P))
-        first_norm_stats(2)
-        first_norm_stats(3)
-        quantise_chunk(11)
-        quantise_hn(0)
-        quantise_hn(1)
-        first_norm_apply(2)
-        first_norm_apply(3)
-        stage2(0)
-        transpose_hn(2)
-        transpose_hn(3)
-        second_norm_stats(0)
-        second_norm_stats(1)
-        quantise_hn(2)
-        quantise_hn(3)
-        second_norm_apply(0)
-        second_norm_apply(1)
-        stage2(1)
-        second_norm_stats(2)
-        second_norm_stats(3)
-        second_norm_apply(2)
-        second_norm_apply(3)
+        stages = [
+            add_ent, first_norm_centre, first_norm_scale, transpose_hn, round_hn, quantise_hn, stage2,
+            transpose_interf, add_hn, second_norm_centre, second_norm_scale,
+        ]
+        for r in range(len(stages) + TILE_SKEW * (TOKEN_TILES - 1)):
+            if ENT_PASSES + 1 + r <= len(chunks):
+                weight_step(ENT_PASSES + 1 + r)
+            for tt in reversed(range(TOKEN_TILES)):
+                s = r - TILE_SKEW * tt
+                if 0 <= s < len(stages):
+                    stages[s](tt)

@@ -77,17 +77,13 @@ def tile_quantuminspiredneuralcore_pb_kernel(
             cols = slice(half * (K_ENT // 2), (half + 1) * (K_ENT // 2))
             nc.sync.dma_start(out=e_raw[tt][:, cols], in_=e_rows[tt * P : (tt + 1) * P, cols])
 
-        load_e(0, 0)
+        nc.sync.dma_start(out=h_sb[:], in_=h_rows.rearrange("(t p) f -> p t f", p=P))
         nc.sync.dma_start(out=ent_pb_rows[0:1, :], in_=ent_pb.unsqueeze(0))
         nc.sync.dma_start(out=vec_rows[0:1, :], in_=ln3_g.unsqueeze(0))
         nc.sync.dma_start(out=vec_rows[1:2, :], in_=ln3_b.unsqueeze(0))
         nc.sync.dma_start(out=vec_rows[2:4, :], in_=path_b)
         nc.sync.dma_start(out=vec_rows[4:6, :], in_=phase)
-        load_e(0, 1)
-        load_e(1, 0)
-        load_e(1, 1)
-        nc.sync.dma_start(out=h_sb[:], in_=h_rows.rearrange("(t p) f -> p t f", p=P))
-        for tt in range(2, TOKEN_TILES):
+        for tt in range(TOKEN_TILES):
             load_e(tt, 0)
             load_e(tt, 1)
         table_warm = consts.tile([P, 1], F32)
@@ -104,6 +100,9 @@ def tile_quantuminspiredneuralcore_pb_kernel(
             return spread
 
         ent_pb_spread = spread_row(ent_pb_rows, 0, "ent_pb_spread")
+        x_all = keep.tile([P, TOKEN_TILES, FEATURES], F32)
+        for tt in range(TOKEN_TILES):
+            nc.gpsimd.tensor_tensor(out=x_all[:, tt, :], in0=h_sb[:, tt, :], in1=ent_pb_spread[:], op=ALU.add)
         ln3_g_spread = spread_row(vec_rows, 0, "ln3_g_spread")
         ln3_b_spread = spread_row(vec_rows, 1, "ln3_b_spread")
 
@@ -140,10 +139,6 @@ def tile_quantuminspiredneuralcore_pb_kernel(
         nc.vector.tensor_tensor(out=bias_mod[:], in0=path_b_cols[:], in1=mod[:], op=ALU.mult)
         bias_sum = consts.tile([P, FEATURE_TILES], F32)
         nc.vector.tensor_tensor(out=bias_sum[:], in0=bias_mod[:, 0, :], in1=bias_mod[:, 1, :], op=ALU.add)
-
-        x_all = keep.tile([P, TOKEN_TILES, FEATURES], F32)
-        for tt in range(TOKEN_TILES):
-            nc.gpsimd.tensor_tensor(out=x_all[:, tt, :], in0=h_sb[:, tt, :], in1=ent_pb_spread[:], op=ALU.add)
 
         hn_all = keep.tile([P, TOKEN_TILES, FEATURES], F32)
         hn_grouped = keep.tile([P, TOKEN_TILES, PATH_PASSES, P, PACK], BF16, align_bytes=64)
@@ -271,7 +266,7 @@ def tile_quantuminspiredneuralcore_pb_kernel(
 
         def scale_and_shift(tt, dst, shift):
             nc.vector.scalar_tensor_tensor(
-                out=dst, in0=dst, scalar=rstd[tt][:], in1=shift[:], op0=ALU.mult, op1=ALU.add
+                out=dst, in0=dst, scalar=rstd[tt][:], in1=shift, op0=ALU.mult, op1=ALU.add
             )
 
         def add_ent(tt):
@@ -282,7 +277,7 @@ def tile_quantuminspiredneuralcore_pb_kernel(
             centre_and_gain(tt, hn_all[:, tt, :], x_all[:, tt, :], ln3_g_spread)
 
         def first_norm_scale(tt):
-            scale_and_shift(tt, hn_all[:, tt, :], ln3_b_spread)
+            scale_and_shift(tt, hn_all[:, tt, :], ln3_b_spread[:])
 
         def transpose_hn(tt):
             hn_banks[tt] = []
@@ -350,8 +345,10 @@ def tile_quantuminspiredneuralcore_pb_kernel(
             centre_and_gain(tt, hn_all[:, tt, :], x_all[:, tt, :], ln4_g_spread)
 
         def second_norm_scale(tt):
-            scale_and_shift(tt, hn_all[:, tt, :], ln4_b_spread)
-            nc.sync.dma_start(out=out_rows[tt * P : (tt + 1) * P, :], in_=hn_all[:, tt, :])
+            for half in range(HALVES):
+                cols = slice(half * BANK, (half + 1) * BANK)
+                scale_and_shift(tt, hn_all[:, tt, cols], ln4_b_spread[:, cols])
+                nc.sync.dma_start(out=out_rows[tt * P : (tt + 1) * P, cols], in_=hn_all[:, tt, cols])
 
         stages = [
             add_ent, first_norm_centre, first_norm_scale, transpose_hn, round_hn, quantise_hn, stage2,

@@ -77,13 +77,17 @@ def tile_quantuminspiredneuralcore_pb_kernel(
             cols = slice(half * (K_ENT // 2), (half + 1) * (K_ENT // 2))
             nc.sync.dma_start(out=e_raw[tt][:, cols], in_=e_rows[tt * P : (tt + 1) * P, cols])
 
-        nc.sync.dma_start(out=h_sb[:], in_=h_rows.rearrange("(t p) f -> p t f", p=P))
+        load_e(0, 0)
         nc.sync.dma_start(out=ent_pb_rows[0:1, :], in_=ent_pb.unsqueeze(0))
         nc.sync.dma_start(out=vec_rows[0:1, :], in_=ln3_g.unsqueeze(0))
         nc.sync.dma_start(out=vec_rows[1:2, :], in_=ln3_b.unsqueeze(0))
         nc.sync.dma_start(out=vec_rows[2:4, :], in_=path_b)
         nc.sync.dma_start(out=vec_rows[4:6, :], in_=phase)
-        for tt in range(TOKEN_TILES):
+        load_e(0, 1)
+        load_e(1, 0)
+        load_e(1, 1)
+        nc.sync.dma_start(out=h_sb[:], in_=h_rows.rearrange("(t p) f -> p t f", p=P))
+        for tt in range(2, TOKEN_TILES):
             load_e(tt, 0)
             load_e(tt, 1)
         table_warm = consts.tile([P, 1], F32)
@@ -100,9 +104,6 @@ def tile_quantuminspiredneuralcore_pb_kernel(
             return spread
 
         ent_pb_spread = spread_row(ent_pb_rows, 0, "ent_pb_spread")
-        x_all = keep.tile([P, TOKEN_TILES, FEATURES], F32)
-        for tt in range(TOKEN_TILES):
-            nc.gpsimd.tensor_tensor(out=x_all[:, tt, :], in0=h_sb[:, tt, :], in1=ent_pb_spread[:], op=ALU.add)
         ln3_g_spread = spread_row(vec_rows, 0, "ln3_g_spread")
         ln3_b_spread = spread_row(vec_rows, 1, "ln3_b_spread")
 
@@ -140,6 +141,8 @@ def tile_quantuminspiredneuralcore_pb_kernel(
         bias_sum = consts.tile([P, FEATURE_TILES], F32)
         nc.vector.tensor_tensor(out=bias_sum[:], in0=bias_mod[:, 0, :], in1=bias_mod[:, 1, :], op=ALU.add)
 
+        x_all = keep.tile([P, TOKEN_TILES, FEATURES], F32)
+
         hn_all = keep.tile([P, TOKEN_TILES, FEATURES], F32)
         hn_grouped = keep.tile([P, TOKEN_TILES, PATH_PASSES, P, PACK], BF16, align_bytes=64)
         hn_codes = keep.tile([P, TOKEN_TILES, PATH_PASSES, P], U32, align_bytes=64)
@@ -165,11 +168,10 @@ def tile_quantuminspiredneuralcore_pb_kernel(
                         for u in range(2):
                             first = (2 * pair + c2) * 2 * P + u * P
                             nc.tensor.transpose(bank[:, c2, u, :], e_words[:, first : first + P], ident_f32[:])
-                    planes = bank[:].rearrange("p c u r -> p c r u")
-                    if pair < 3:
-                        nc.scalar.copy(out=grouped_words[:, 2 * pair : 2 * pair + 2], in_=planes)
-                    else:
-                        nc.vector.tensor_copy(out=grouped_words[:, 2 * pair : 2 * pair + 2], in_=planes)
+                    nc.scalar.copy(
+                        out=grouped_words[:, 2 * pair : 2 * pair + 2], in_=bank[:].rearrange("p c u r -> p c r u")
+                    )
+                nc.vector.tensor_tensor(out=x_all[:, tt, :], in0=h_sb[:, tt, :], in1=ent_pb_spread[:], op=ALU.add)
                 nc.vector.quantize_mx(
                     out=e_codes[:, tt].rearrange("p c r -> p (c r)").bitcast(FP8X4),
                     scales=e_scales[:, tt].rearrange("p c r -> p (c r)"),
@@ -266,7 +268,7 @@ def tile_quantuminspiredneuralcore_pb_kernel(
 
         def scale_and_shift(tt, dst, shift):
             nc.vector.scalar_tensor_tensor(
-                out=dst, in0=dst, scalar=rstd[tt][:], in1=shift, op0=ALU.mult, op1=ALU.add
+                out=dst, in0=dst, scalar=rstd[tt][:], in1=shift[:], op0=ALU.mult, op1=ALU.add
             )
 
         def add_ent(tt):
@@ -277,7 +279,7 @@ def tile_quantuminspiredneuralcore_pb_kernel(
             centre_and_gain(tt, hn_all[:, tt, :], x_all[:, tt, :], ln3_g_spread)
 
         def first_norm_scale(tt):
-            scale_and_shift(tt, hn_all[:, tt, :], ln3_b_spread[:])
+            scale_and_shift(tt, hn_all[:, tt, :], ln3_b_spread)
 
         def transpose_hn(tt):
             hn_banks[tt] = []
@@ -345,10 +347,8 @@ def tile_quantuminspiredneuralcore_pb_kernel(
             centre_and_gain(tt, hn_all[:, tt, :], x_all[:, tt, :], ln4_g_spread)
 
         def second_norm_scale(tt):
-            for half in range(HALVES):
-                cols = slice(half * BANK, (half + 1) * BANK)
-                scale_and_shift(tt, hn_all[:, tt, cols], ln4_b_spread[:, cols])
-                nc.sync.dma_start(out=out_rows[tt * P : (tt + 1) * P, cols], in_=hn_all[:, tt, cols])
+            scale_and_shift(tt, hn_all[:, tt, :], ln4_b_spread)
+            nc.sync.dma_start(out=out_rows[tt * P : (tt + 1) * P, :], in_=hn_all[:, tt, :])
 
         stages = [
             add_ent, first_norm_centre, first_norm_scale, transpose_hn, round_hn, quantise_hn, stage2,

@@ -30,7 +30,8 @@ PATHS = 2
 PATH_PASSES = FEATURES // K_PASS
 EPS = 1e-5
 
-VECTOR_COLS = FEATURES // 2
+ENT_VECTOR_COLS = 512
+PATH_VECTOR_COLS = 384
 
 TILE_SKEW = 2
 
@@ -200,7 +201,7 @@ def tile_quantuminspiredneuralcore_pb_kernel(
                     grouped[i] = grouped_pool.tile([P, FEATURES, PACK], BF16, tag="grouped", name="w_grouped", align_bytes=64)
                     src = raw[:].rearrange("p (t c i) -> p c t i", t=PACK, i=4)
                     dst = grouped[i][:].rearrange("p (c i) t -> p c t i", i=4)
-                    split = VECTOR_COLS // 4
+                    split = (ENT_VECTOR_COLS if i < ENT_PASSES else PATH_VECTOR_COLS) // 4
                     nc.vector.tensor_copy(out=dst[:, :split], in_=src[:, :split])
                     nc.scalar.copy(out=dst[:, split:], in_=src[:, split:])
                 if i == len(chunks) - 1:
@@ -268,7 +269,7 @@ def tile_quantuminspiredneuralcore_pb_kernel(
 
         def scale_and_shift(tt, dst, shift):
             nc.vector.scalar_tensor_tensor(
-                out=dst, in0=dst, scalar=rstd[tt][:], in1=shift[:], op0=ALU.mult, op1=ALU.add
+                out=dst, in0=dst, scalar=rstd[tt][:], in1=shift, op0=ALU.mult, op1=ALU.add
             )
 
         def add_ent(tt):
@@ -279,7 +280,7 @@ def tile_quantuminspiredneuralcore_pb_kernel(
             centre_and_gain(tt, hn_all[:, tt, :], x_all[:, tt, :], ln3_g_spread)
 
         def first_norm_scale(tt):
-            scale_and_shift(tt, hn_all[:, tt, :], ln3_b_spread)
+            scale_and_shift(tt, hn_all[:, tt, :], ln3_b_spread[:])
 
         def transpose_hn(tt):
             hn_banks[tt] = []
@@ -347,8 +348,10 @@ def tile_quantuminspiredneuralcore_pb_kernel(
             centre_and_gain(tt, hn_all[:, tt, :], x_all[:, tt, :], ln4_g_spread)
 
         def second_norm_scale(tt):
-            scale_and_shift(tt, hn_all[:, tt, :], ln4_b_spread)
-            nc.sync.dma_start(out=out_rows[tt * P : (tt + 1) * P, :], in_=hn_all[:, tt, :])
+            for half in range(HALVES):
+                cols = slice(half * BANK, (half + 1) * BANK)
+                scale_and_shift(tt, hn_all[:, tt, cols], ln4_b_spread[:, cols])
+                nc.sync.dma_start(out=out_rows[tt * P : (tt + 1) * P, cols], in_=hn_all[:, tt, cols])
 
         stages = [
             add_ent, first_norm_centre, first_norm_scale, transpose_hn, round_hn, quantise_hn, stage2,

@@ -17,7 +17,7 @@ P = 128
 PACK = 4
 K_PASS = P * PACK
 BANK = 512
-PSUM_BANKS = 8
+RING = 4
 
 TOKENS = 512
 TOKEN_TILES = TOKENS // P
@@ -30,10 +30,14 @@ PATHS = 2
 PATH_PASSES = FEATURES // K_PASS
 EPS = 1e-5
 
-ENT_VECTOR_COLS = 512
-PATH_VECTOR_COLS = 384
+BLOCKS = [
+    ("e", 0), ("e", 1), ("e", 2), ("e", 3), ("ent", 0), ("ent", 1), ("ent", 2), ("ent", 3), ("ent", 4), ("ent", 5), ("ent", 6), ("ent", 7), ("path", 0), ("path", 1), ("path", 2), ("path", 3),
+]
+RAW_BUFS = 6
+GROUPED_BUFS = 3
 
-TILE_SKEW = 2
+ENT_VECTOR_COLS = 480
+PATH_VECTOR_COLS = 512
 
 TWO_PI_HEAD = 6.28125
 TWO_PI_REST = 2.0 * math.pi - TWO_PI_HEAD
@@ -56,9 +60,9 @@ def tile_quantuminspiredneuralcore_pb_kernel(
         keep = ctx.enter_context(tc.tile_pool(name="keep", bufs=1))
         stats = ctx.enter_context(tc.tile_pool(name="stats", bufs=TOKEN_TILES))
         scratch = ctx.enter_context(tc.tile_pool(name="scratch", bufs=2))
-        raw_pool = ctx.enter_context(tc.tile_pool(name="raw", bufs=5))
-        grouped_pool = ctx.enter_context(tc.tile_pool(name="grouped", bufs=3))
-        psum = ctx.enter_context(tc.psum_pool(name="psum", bufs=PSUM_BANKS))
+        raw_pool = ctx.enter_context(tc.tile_pool(name="raw", bufs=RAW_BUFS))
+        grouped_pool = ctx.enter_context(tc.tile_pool(name="grouped", bufs=GROUPED_BUFS))
+        psum = ctx.enter_context(tc.psum_pool(name="psum", bufs=RING))
 
         ident_f32 = consts.tile([P, P], F32)
         make_identity(nc, ident_f32[:])
@@ -70,247 +74,267 @@ def tile_quantuminspiredneuralcore_pb_kernel(
         nc.vector.memset(vec_rows[:].bitcast(I32), 0)
         ident_bf16 = consts.tile([P, P], BF16)
         nc.vector.tensor_copy(out=ident_bf16[:], in_=ident_f32[:])
+        table_warm = consts.tile([P, 1], F32)
 
         h_sb = keep.tile([P, TOKEN_TILES, FEATURES], BF16)
-        e_raw = [raw_pool.tile([P, K_ENT], BF16, tag="raw", name="e_raw_%d" % tt) for tt in range(TOKEN_TILES)]
-
-        def load_e(tt, half):
-            cols = slice(half * (K_ENT // 2), (half + 1) * (K_ENT // 2))
-            nc.sync.dma_start(out=e_raw[tt][:, cols], in_=e_rows[tt * P : (tt + 1) * P, cols])
-
-        load_e(0, 0)
-        nc.sync.dma_start(out=ent_pb_rows[0:1, :], in_=ent_pb.unsqueeze(0))
-        nc.sync.dma_start(out=vec_rows[0:1, :], in_=ln3_g.unsqueeze(0))
-        nc.sync.dma_start(out=vec_rows[1:2, :], in_=ln3_b.unsqueeze(0))
-        nc.sync.dma_start(out=vec_rows[2:4, :], in_=path_b)
-        nc.sync.dma_start(out=vec_rows[4:6, :], in_=phase)
-        load_e(0, 1)
-        load_e(1, 0)
-        load_e(1, 1)
-        nc.sync.dma_start(out=h_sb[:], in_=h_rows.rearrange("(t p) f -> p t f", p=P))
-        for tt in range(2, TOKEN_TILES):
-            load_e(tt, 0)
-            load_e(tt, 1)
-        table_warm = consts.tile([P, 1], F32)
-        nc.scalar.activation(out=table_warm[:], in_=eps[:], func=ACT.Sin)
-
-        def spread_row(rows, r, name):
-            pick_row = ident_bf16[:, r : r + 1].to_broadcast([P, P])
-            bank = psum.tile([P, FEATURES], BF16, tag="bank")
-            for half in range(HALVES):
-                cols = slice(half * BANK, (half + 1) * BANK)
-                nc.tensor.matmul(out=bank[:, cols], lhsT=pick_row, rhs=rows[:, cols], start=True, stop=True)
-            spread = consts.tile([P, FEATURES], BF16, name=name)
-            nc.scalar.copy(out=spread[:], in_=bank[:])
-            return spread
-
-        ent_pb_spread = spread_row(ent_pb_rows, 0, "ent_pb_spread")
-        ln3_g_spread = spread_row(vec_rows, 0, "ln3_g_spread")
-        ln3_b_spread = spread_row(vec_rows, 1, "ln3_b_spread")
-
-        cols_bank = psum.tile([P, FEATURE_TILES, P], BF16, tag="bank")
-        for j in range(FEATURE_TILES):
-            nc.tensor.transpose(cols_bank[:, j, :], vec_rows[:, j * P : (j + 1) * P], ident_bf16[:])
-        path_b_cols = consts.tile([P, PATHS, FEATURE_TILES], F32)
-        nc.vector.tensor_copy(out=path_b_cols[:], in_=cols_bank[:, :, 2:4].rearrange("p j r -> p r j"))
-        phase_cols = consts.tile([P, PATHS, FEATURE_TILES], F32)
-        nc.vector.tensor_copy(out=phase_cols[:], in_=cols_bank[:, :, 4:6].rearrange("p j r -> p r j"))
-
-        turns = consts.tile([P, PATHS, FEATURE_TILES], F32)
-        nc.vector.tensor_scalar(
-            out=turns[:], in0=phase_cols[:], scalar1=1.0 / (2.0 * math.pi), scalar2=ROUND_TO_INT,
-            op0=ALU.mult, op1=ALU.add,
-        )
-        nc.vector.tensor_scalar(out=turns[:], in0=turns[:], scalar1=ROUND_TO_INT, scalar2=None, op0=ALU.subtract)
-        angle = consts.tile([P, PATHS, FEATURE_TILES], F32)
-        nc.vector.scalar_tensor_tensor(
-            out=angle[:], in0=turns[:], scalar=-TWO_PI_HEAD, in1=phase_cols[:], op0=ALU.mult, op1=ALU.add
-        )
-        nc.vector.scalar_tensor_tensor(
-            out=angle[:], in0=turns[:], scalar=-TWO_PI_REST, in1=angle[:], op0=ALU.mult, op1=ALU.add
-        )
-        sin_full = consts.tile([P, PATHS, FEATURE_TILES], F32)
-        nc.scalar.activation(out=sin_full[:], in_=angle[:], func=ACT.Sin)
-        sin_half = consts.tile([P, PATHS, FEATURE_TILES], F32)
-        nc.scalar.activation(out=sin_half[:], in_=angle[:], func=ACT.Sin, scale=0.5)
-        mod = consts.tile([P, PATHS, FEATURE_TILES], F32)
-        nc.vector.tensor_tensor(out=mod[:], in0=sin_half[:], in1=sin_half[:], op=ALU.mult)
-        nc.vector.tensor_scalar(out=mod[:], in0=mod[:], scalar1=-2.0, scalar2=1.0, op0=ALU.mult, op1=ALU.add)
-        nc.vector.tensor_tensor(out=mod[:], in0=mod[:], in1=sin_full[:], op=ALU.add)
-        bias_mod = consts.tile([P, PATHS, FEATURE_TILES], F32)
-        nc.vector.tensor_tensor(out=bias_mod[:], in0=path_b_cols[:], in1=mod[:], op=ALU.mult)
-        bias_sum = consts.tile([P, FEATURE_TILES], F32)
-        nc.vector.tensor_tensor(out=bias_sum[:], in0=bias_mod[:, 0, :], in1=bias_mod[:, 1, :], op=ALU.add)
-
         x_all = keep.tile([P, TOKEN_TILES, FEATURES], F32)
-
-        hn_all = keep.tile([P, TOKEN_TILES, FEATURES], F32)
-        hn_grouped = keep.tile([P, TOKEN_TILES, PATH_PASSES, P, PACK], BF16, align_bytes=64)
+        hn_t = keep.tile([P, FEATURE_TILES, TOKENS], F32)
+        hn_grouped = keep.tile([P, TOKEN_TILES, PATH_PASSES, P * PACK], BF16, align_bytes=64)
         hn_codes = keep.tile([P, TOKEN_TILES, PATH_PASSES, P], U32, align_bytes=64)
         hn_scales = keep.tile([P, TOKEN_TILES, PATH_PASSES, P], U8, align_bytes=64)
         w2_codes = keep.tile([P, PATHS, PATH_PASSES, FEATURES], U32, align_bytes=64)
         w2_scales = keep.tile([P, PATHS, PATH_PASSES, FEATURES], U8, align_bytes=64)
         ln4_g_spread = consts.tile([P, FEATURES], BF16)
         ln4_b_spread = consts.tile([P, FEATURES], BF16)
+        ent_pb_spread = consts.tile([P, FEATURES], BF16)
+        VECS = 6
+        vec_cols = consts.tile([P, VECS, FEATURE_TILES], F32)
+        ln3_g_cols, ln3_b_cols = vec_cols[:, 0, :], vec_cols[:, 1, :]
+        path_b_cols, phase_cols = vec_cols[:, 2:4, :], vec_cols[:, 4:6, :]
+        turns = consts.tile([P, PATHS, FEATURE_TILES], F32)
+        angle = consts.tile([P, PATHS, FEATURE_TILES], F32)
+        sin_full = consts.tile([P, PATHS, FEATURE_TILES], F32)
+        sin_half = consts.tile([P, PATHS, FEATURE_TILES], F32)
+        mod = consts.tile([P, PATHS, FEATURE_TILES], F32)
+        bias_mod = consts.tile([P, PATHS, FEATURE_TILES], F32)
+        bias_sum = consts.tile([P, FEATURE_TILES], F32)
 
-        with tc.tile_pool(name="stage1", bufs=1) as stage1:
-            e_codes = stage1.tile([P, TOKEN_TILES, ENT_PASSES, P], U32, align_bytes=64)
-            e_scales = stage1.tile([P, TOKEN_TILES, ENT_PASSES, P], U8, align_bytes=64)
-            w1_codes = stage1.tile([P, ENT_PASSES, FEATURES], U32, align_bytes=64)
-            w1_scales = stage1.tile([P, ENT_PASSES, FEATURES], U8, align_bytes=64)
+        tasks = {}
+        done = set()
+        raw, grouped, memory = {}, {}, {}
+        emptied_by = {"left": [], "right": []}
 
-            for tt in range(TOKEN_TILES):
-                e_words = e_raw[tt][:].bitcast(F32)
-                e_grouped = grouped_pool.tile([P, K_ENT], BF16, tag="grouped", align_bytes=64)
-                grouped_words = e_grouped[:].bitcast(F32).rearrange("p (c r u) -> p c r u", c=ENT_PASSES, u=2)
-                for pair in range(ENT_PASSES // 2):
-                    bank = psum.tile([P, 2, 2, P], F32, tag="bank")
-                    for c2 in range(2):
-                        for u in range(2):
-                            first = (2 * pair + c2) * 2 * P + u * P
-                            nc.tensor.transpose(bank[:, c2, u, :], e_words[:, first : first + P], ident_f32[:])
-                    nc.scalar.copy(
-                        out=grouped_words[:, 2 * pair : 2 * pair + 2], in_=bank[:].rearrange("p c u r -> p c r u")
-                    )
-                nc.vector.tensor_tensor(out=x_all[:, tt, :], in0=h_sb[:, tt, :], in1=ent_pb_spread[:], op=ALU.add)
-                nc.vector.quantize_mx(
-                    out=e_codes[:, tt].rearrange("p c r -> p (c r)").bitcast(FP8X4),
-                    scales=e_scales[:, tt].rearrange("p c r -> p (c r)"),
-                    in_=e_grouped[:],
+        def bank(ring, shape, dtype, reader):
+            emptied_by[ring].append(reader)
+            return psum.tile(shape, dtype, tag=ring, name=ring + "_bank")
+
+        def banks_free(ring, count):
+            return all(r in done for r in emptied_by[ring][-RING:][:max(0, count - max(0, RING - len(emptied_by[ring])))])
+
+        def weight_rows(kind, index):
+            if kind == "ent":
+                chunk = ent_pw[index * K_PASS : (index + 1) * K_PASS, :]
+                return chunk.rearrange("(u p s) n -> p u (s n)", u=2, s=2)
+            path, c = divmod(index, PATH_PASSES)
+            return path_w[path, c * K_PASS : (c + 1) * K_PASS, :].rearrange("(t p) n -> p t n", p=P)
+
+        def load(i):
+            kind, index = BLOCKS[i]
+            raw[i] = raw_pool.tile([P, K_ENT], BF16, tag="raw", name="raw")
+            if kind == "e":
+                parts = 2 if index == 0 else 1
+                for part in range(parts):
+                    cols = slice(part * (K_ENT // parts), (part + 1) * (K_ENT // parts))
+                    nc.sync.dma_start(out=raw[i][:, cols], in_=e_rows[index * P : (index + 1) * P, cols])
+            else:
+                rows = weight_rows(kind, index)
+                nc.sync.dma_start(out=raw[i][:].rearrange("p (a b) -> p a b", a=rows.shape[1]), in_=rows)
+
+        def load_h(tt):
+            nc.sync.dma_start(out=h_sb[:, tt, :], in_=h_rows[tt * P : (tt + 1) * P, :])
+
+        def load_vectors():
+            nc.scalar.dma_start(out=ent_pb_rows[0:1, :], in_=ent_pb.unsqueeze(0))
+            nc.scalar.dma_start(out=vec_rows[0:1, :], in_=ln3_g.unsqueeze(0))
+            nc.scalar.dma_start(out=vec_rows[1:2, :], in_=ln3_b.unsqueeze(0))
+            nc.scalar.dma_start(out=vec_rows[2:4, :], in_=path_b)
+            nc.scalar.dma_start(out=vec_rows[4:6, :], in_=phase)
+
+        def load_ln4():
+            nc.sync.dma_start(out=ln4_g_spread[:], in_=ln4_g.partition_broadcast(P))
+            nc.sync.dma_start(out=ln4_b_spread[:], in_=ln4_b.partition_broadcast(P))
+
+        def grouped_tile(i):
+            if i not in grouped:
+                grouped[i] = grouped_pool.tile([P, K_ENT], BF16, tag="grouped", name="grouped", align_bytes=64)
+            return grouped[i]
+
+        def transpose_e(i):
+            e_words = raw[i][:].bitcast(F32)
+            memory["e", i] = []
+            for pair in range(ENT_PASSES // 2):
+                e_bank = bank("right", [P, 2, 2, P], F32, ("empty_e", i))
+                for c2 in range(2):
+                    for u in range(2):
+                        first = (2 * pair + c2) * 2 * P + u * P
+                        nc.tensor.transpose(e_bank[:, c2, u, :], e_words[:, first : first + P], ident_f32[:])
+                memory["e", i].append(e_bank)
+
+        def empty_e(i):
+            grouped_words = grouped_tile(i)[:].bitcast(F32).rearrange("p (c r u) -> p c r u", c=ENT_PASSES, u=2)
+            for pair, e_bank in enumerate(memory["e", i]):
+                nc.scalar.copy(
+                    out=grouped_words[:, 2 * pair : 2 * pair + 2], in_=e_bank[:].rearrange("p c u r -> p c r u")
                 )
 
-            chunks = []
-            for c in range(ENT_PASSES):
-                rows = ent_pw[c * K_PASS : (c + 1) * K_PASS, :].rearrange("(u p s) n -> p u (s n)", u=2, s=2)
-                chunks.append((rows, w1_codes[:, c, :], w1_scales[:, c, :]))
-            for path in range(PATHS):
-                for c in range(PATH_PASSES):
-                    rows = path_w[path, c * K_PASS : (c + 1) * K_PASS, :].rearrange("(t p) n -> p t n", p=P)
-                    chunks.append((rows, w2_codes[:, path, c, :], w2_scales[:, path, c, :]))
-            grouped = {}
-            ent_acc = [
-                [psum.tile([P, BANK], F32, tag="bank", name="ent_acc_%d_%d" % (tt, half)) for half in range(HALVES)]
-                for tt in range(TOKEN_TILES)
-            ]
+        def regroup(i, copy, first, last):
+            src = raw[i][:].rearrange("p (t c i) -> p c t i", t=PACK, i=4)
+            dst = grouped_tile(i)[:].rearrange("p (c i t) -> p c t i", i=4, t=PACK)
+            copy(out=dst[:, first // 4 : last // 4], in_=src[:, first // 4 : last // 4])
 
-            def weight_step(i):
-                if i < len(chunks):
-                    rows = chunks[i][0]
-                    raw = raw_pool.tile([P, PACK * FEATURES], BF16, tag="raw")
-                    nc.sync.dma_start(out=raw[:].rearrange("p (a b) -> p a b", a=rows.shape[1]), in_=rows)
-                    grouped[i] = grouped_pool.tile([P, FEATURES, PACK], BF16, tag="grouped", name="w_grouped", align_bytes=64)
-                    src = raw[:].rearrange("p (t c i) -> p c t i", t=PACK, i=4)
-                    dst = grouped[i][:].rearrange("p (c i) t -> p c t i", i=4)
-                    split = (ENT_VECTOR_COLS if i < ENT_PASSES else PATH_VECTOR_COLS) // 4
-                    nc.vector.tensor_copy(out=dst[:, :split], in_=src[:, :split])
-                    nc.scalar.copy(out=dst[:, split:], in_=src[:, split:])
-                if i == len(chunks) - 1:
-                    nc.sync.dma_start(out=ln4_g_spread[:], in_=ln4_g.partition_broadcast(P))
-                    nc.sync.dma_start(out=ln4_b_spread[:], in_=ln4_b.partition_broadcast(P))
-                if i == 0:
-                    return
-                c = i - 1
-                nc.vector.quantize_mx(
-                    out=chunks[c][1].bitcast(FP8X4), scales=chunks[c][2], in_=grouped[c][:].rearrange("p n t -> p (n t)")
+        def vector_cols(i):
+            kind, index = BLOCKS[i]
+            if kind == "path":
+                return PATH_VECTOR_COLS
+            return ENT_VECTOR_COLS
+
+        def quantise(i):
+            kind, index = BLOCKS[i]
+            if kind == "e":
+                codes = e_codes[:, index].rearrange("p c r -> p (c r)")
+                scales = e_scales[:, index].rearrange("p c r -> p (c r)")
+            elif kind == "ent":
+                codes, scales = w1_codes[:, index, :], w1_scales[:, index, :]
+            else:
+                path, c = divmod(index, PATH_PASSES)
+                codes, scales = w2_codes[:, path, c, :], w2_scales[:, path, c, :]
+            nc.vector.quantize_mx(out=codes.bitcast(FP8X4), scales=scales, in_=grouped[i][:])
+
+        def multiply(c, tt):
+            if ("acc", tt) not in memory:
+                ring = "left" if tt < TOKEN_TILES // 2 else "right"
+                memory["acc", tt] = [bank(ring, [P, BANK], F32, ("add_ent", tt)) for half in range(HALVES)]
+            for half in range(HALVES):
+                cols = slice(half * BANK, (half + 1) * BANK)
+                nc.tensor.matmul_mx(
+                    out=memory["acc", tt][half][:],
+                    lhsT=e_codes[:, tt, c, :].bitcast(FP8X4),
+                    lhsT_scale=e_scales[:, tt, c, :],
+                    rhs=w1_codes[:, c, cols].bitcast(FP8X4),
+                    rhs_scale=w1_scales[:, c, cols],
+                    start=(c == 0),
+                    stop=(c == ENT_PASSES - 1),
                 )
-                if c >= ENT_PASSES:
-                    return
-                for tt in range(TOKEN_TILES):
-                    for half in range(HALVES):
-                        cols = slice(half * BANK, (half + 1) * BANK)
-                        nc.tensor.matmul_mx(
-                            out=ent_acc[tt][half][:],
-                            lhsT=e_codes[:, tt, c, :].bitcast(FP8X4),
-                            lhsT_scale=e_scales[:, tt, c, :],
-                            rhs=w1_codes[:, c, cols].bitcast(FP8X4),
-                            rhs_scale=w1_scales[:, c, cols],
-                            start=(c == 0),
-                            stop=(c == ENT_PASSES - 1),
-                        )
 
-            for i in range(ENT_PASSES + 1):
-                weight_step(i)
+        def spread_ent_pb():
+            pick_row = ident_bf16[:, 0:1].to_broadcast([P, P])
+            memory["pb"] = bank("right", [P, FEATURES], BF16, "copy_ent_pb")
+            for half in range(HALVES):
+                cols = slice(half * BANK, (half + 1) * BANK)
+                nc.tensor.matmul(out=memory["pb"][:, cols], lhsT=pick_row, rhs=ent_pb_rows[:, cols], start=True, stop=True)
 
-        tail = ctx.enter_context(tc.tile_pool(name="tail", bufs=1))
-        interf_t = tail.tile([P, PATHS, FEATURE_TILES, TOKENS], F32)
+        def copy_ent_pb():
+            nc.scalar.copy(out=ent_pb_spread[:], in_=memory["pb"][:])
 
-        row_sums, neg_mean, rstd, hn_banks, y_banks = {}, {}, {}, {}, {}
+        def turn_vectors():
+            memory["cols"] = bank("right", [P, FEATURE_TILES, P], BF16, "copy_vectors")
+            for j in range(FEATURE_TILES):
+                nc.tensor.transpose(memory["cols"][:, j, :], vec_rows[:, j * P : (j + 1) * P], ident_bf16[:])
 
-        def add_and_sum(tt, dst, banks, addend):
-            row_sums[tt] = stats.tile([P, HALVES], F32, name="row_sums")
+        def copy_vectors():
+            nc.vector.tensor_copy(out=vec_cols[:], in_=memory["cols"][:, :, 0:VECS].rearrange("p j r -> p r j"))
+
+        def sines():
+            nc.scalar.activation(out=sin_full[:], in_=angle[:], func=ACT.Sin)
+            nc.scalar.activation(out=sin_half[:], in_=angle[:], func=ACT.Sin, scale=0.5)
+
+        chores = [
+            lambda: nc.vector.tensor_scalar(
+                out=turns[:], in0=phase_cols, scalar1=1.0 / (2.0 * math.pi), scalar2=ROUND_TO_INT,
+                op0=ALU.mult, op1=ALU.add,
+            ),
+            lambda: nc.vector.tensor_scalar(
+                out=turns[:], in0=turns[:], scalar1=ROUND_TO_INT, scalar2=None, op0=ALU.subtract
+            ),
+            lambda: nc.vector.scalar_tensor_tensor(
+                out=angle[:], in0=turns[:], scalar=-TWO_PI_HEAD, in1=phase_cols, op0=ALU.mult, op1=ALU.add
+            ),
+            lambda: nc.vector.scalar_tensor_tensor(
+                out=angle[:], in0=turns[:], scalar=-TWO_PI_REST, in1=angle[:], op0=ALU.mult, op1=ALU.add
+            ),
+            lambda: nc.vector.tensor_tensor(out=mod[:], in0=sin_half[:], in1=sin_half[:], op=ALU.mult),
+            lambda: nc.vector.tensor_scalar(
+                out=mod[:], in0=mod[:], scalar1=-2.0, scalar2=1.0, op0=ALU.mult, op1=ALU.add
+            ),
+            lambda: nc.vector.tensor_tensor(out=mod[:], in0=mod[:], in1=sin_full[:], op=ALU.add),
+            lambda: nc.vector.tensor_tensor(out=bias_mod[:], in0=path_b_cols, in1=mod[:], op=ALU.mult),
+            lambda: nc.vector.tensor_tensor(out=bias_sum[:], in0=bias_mod[:, 0, :], in1=bias_mod[:, 1, :], op=ALU.add),
+        ]
+        SINES_BEHIND = 3
+
+        def start_x(tt):
+            nc.vector.tensor_tensor(out=x_all[:, tt, :], in0=h_sb[:, tt, :], in1=ent_pb_spread[:], op=ALU.add)
+
+        def add_ent(tt):
+            memory["sums", tt] = stats.tile([P, HALVES], F32, name="row_sums")
             for half in range(HALVES):
                 cols = slice(half * BANK, (half + 1) * BANK)
                 nc.vector.scalar_tensor_tensor(
-                    out=dst[:, cols], in0=banks[half][:], scalar=0.0, in1=addend[:, cols],
-                    op0=ALU.add, op1=ALU.add, accum_out=row_sums[tt][:, half : half + 1],
+                    out=x_all[:, tt, cols], in0=memory["acc", tt][half][:], scalar=0.0, in1=x_all[:, tt, cols],
+                    op0=ALU.add, op1=ALU.add, accum_out=memory["sums", tt][:, half : half + 1],
                 )
 
-        def statistics(tt, src):
-            scaled_sums = stats.tile([P, HALVES], F32)
-            neg_mean[tt] = stats.tile([P, 1], F32, name="neg_mean")
+        def mean(tt):
+            scaled_sums = stats.tile([P, HALVES], F32, name="scaled_sums")
+            memory["neg_mean", tt] = stats.tile([P, 1], F32, name="neg_mean")
             nc.scalar.activation(
-                out=scaled_sums[:], in_=row_sums[tt][:], func=ACT.Identity, scale=-1.0 / FEATURES,
-                accum_out=neg_mean[tt][:],
+                out=scaled_sums[:], in_=memory["sums", tt][:], func=ACT.Identity, scale=-1.0 / FEATURES,
+                accum_out=memory["neg_mean", tt][:],
             )
-            squares = scratch.tile([P, FEATURES], BF16)
-            sum_sq = stats.tile([P, 1], F32)
+
+        def squares(tt):
+            squared = scratch.tile([P, FEATURES], BF16, name="squared")
+            memory["sum_sq", tt] = stats.tile([P, 1], F32, name="sum_sq")
             nc.scalar.activation(
-                out=squares[:], in_=src, func=ACT.Square, bias=neg_mean[tt][:], scale=1.0, accum_out=sum_sq[:]
+                out=squared[:], in_=x_all[:, tt, :], func=ACT.Square, bias=memory["neg_mean", tt][:], scale=1.0,
+                accum_out=memory["sum_sq", tt][:],
             )
-            rstd[tt] = stats.tile([P, 1], F32, name="rstd")
+
+        def first_rstd(tt):
+            memory["rstd", tt] = stats.tile([P, 1], F32, name="rstd")
             nc.scalar.activation(
-                out=rstd[tt][:], in_=sum_sq[:], func=ACT.Abs_reciprocal_sqrt, bias=eps[:], scale=1.0 / FEATURES
+                out=memory["rstd", tt][:], in_=memory["sum_sq", tt][:], func=ACT.Abs_reciprocal_sqrt, bias=eps[:],
+                scale=1.0 / FEATURES,
             )
 
-        def centre_and_gain(tt, dst, src, gain):
-            nc.vector.scalar_tensor_tensor(
-                out=dst, in0=src, scalar=neg_mean[tt][:], in1=gain[:], op0=ALU.add, op1=ALU.mult
+        def normalise(tt):
+            nc.vector.tensor_scalar(
+                out=x_all[:, tt, :], in0=x_all[:, tt, :], scalar1=memory["neg_mean", tt][:],
+                scalar2=memory["rstd", tt][:], op0=ALU.add, op1=ALU.mult,
             )
 
-        def scale_and_shift(tt, dst, shift):
-            nc.vector.scalar_tensor_tensor(
-                out=dst, in0=dst, scalar=rstd[tt][:], in1=shift, op0=ALU.mult, op1=ALU.add
-            )
-
-        def add_ent(tt):
-            add_and_sum(tt, x_all[:, tt, :], ent_acc[tt], x_all[:, tt, :])
-
-        def first_norm_centre(tt):
-            statistics(tt, x_all[:, tt, :])
-            centre_and_gain(tt, hn_all[:, tt, :], x_all[:, tt, :], ln3_g_spread)
-
-        def first_norm_scale(tt):
-            scale_and_shift(tt, hn_all[:, tt, :], ln3_b_spread[:])
-
-        def transpose_hn(tt):
-            hn_banks[tt] = []
+        def transpose_z(tt):
+            memory["z", tt] = []
             for c in range(PATH_PASSES):
-                bank = psum.tile([P, PACK, P], F32, tag="bank")
+                z_bank = bank("right", [P, PACK, P], F32, ("gain_shift", tt))
                 for t in range(PACK):
                     first = c * K_PASS + t * P
-                    nc.tensor.transpose(bank[:, t, :], hn_all[:, tt, first : first + P], ident_f32[:])
-                hn_banks[tt].append(bank)
+                    nc.tensor.transpose(z_bank[:, t, :], x_all[:, tt, first : first + P], ident_f32[:])
+                memory["z", tt].append(z_bank)
+
+        def gain_shift(tt):
+            tokens = slice(tt * P, (tt + 1) * P)
+            for j in range(FEATURE_TILES):
+                c, t = divmod(j, PACK)
+                nc.scalar.activation(
+                    out=hn_t[:, j, tokens], in_=memory["z", tt][c][:, t, :], func=ACT.Identity,
+                    scale=ln3_g_cols[:, j : j + 1], bias=ln3_b_cols[:, j : j + 1],
+                )
 
         def round_hn(tt):
+            tokens = slice(tt * P, (tt + 1) * P)
             for c in range(PATH_PASSES):
-                nc.scalar.copy(out=hn_grouped[:, tt, c], in_=hn_banks[tt][c][:].rearrange("p t r -> p r t"))
+                nc.vector.tensor_copy(
+                    out=hn_grouped[:, tt, c].rearrange("p (q i t) -> p q t i", i=4, t=PACK),
+                    in_=hn_t[:, c * PACK : (c + 1) * PACK, tokens].rearrange("p t (q i) -> p q t i", i=4),
+                )
 
         def quantise_hn(tt):
             nc.vector.quantize_mx(
                 out=hn_codes[:, tt].rearrange("p c r -> p (c r)").bitcast(FP8X4),
                 scales=hn_scales[:, tt].rearrange("p c r -> p (c r)"),
-                in_=hn_grouped[:, tt].rearrange("p c r t -> p (c r t)"),
+                in_=hn_grouped[:, tt].rearrange("p c w -> p (c w)"),
             )
 
-        def stage2(tt):
-            tokens = slice(tt * P, (tt + 1) * P)
-            for j in range(FEATURE_TILES):
-                feats = slice(j * P, (j + 1) * P)
-                bank = psum.tile([P, PATHS, P], F32, tag="bank")
-                for path in range(PATHS):
+        def products(tt, path):
+            for quad in range(FEATURE_TILES // 4):
+                t_bank = bank("right", [P, 4, P], F32, ("weigh", tt, path))
+                memory["t", tt, path, quad] = t_bank
+                for k in range(4):
+                    feats = slice((4 * quad + k) * P, (4 * quad + k + 1) * P)
                     for c in range(PATH_PASSES):
                         nc.tensor.matmul_mx(
-                            out=bank[:, path, :],
+                            out=t_bank[:, k, :],
                             lhsT=w2_codes[:, path, c, feats].bitcast(FP8X4),
                             lhsT_scale=w2_scales[:, path, c, feats],
                             rhs=hn_codes[:, tt, c, :].bitcast(FP8X4),
@@ -318,49 +342,199 @@ def tile_quantuminspiredneuralcore_pb_kernel(
                             start=(c == 0),
                             stop=(c == PATH_PASSES - 1),
                         )
-                nc.scalar.activation(
-                    out=interf_t[:, 0, j, tokens], in_=bank[:, 0, :], func=ACT.Identity,
-                    scale=mod[:, 0, j : j + 1], bias=bias_sum[:, j : j + 1],
-                )
-                nc.scalar.activation(
-                    out=interf_t[:, 1, j, tokens], in_=bank[:, 1, :], func=ACT.Identity, scale=mod[:, 1, j : j + 1]
-                )
 
-        def transpose_interf(tt):
+        def weigh(tt, path):
             tokens = slice(tt * P, (tt + 1) * P)
-            y_banks[tt] = []
-            for half in range(HALVES):
-                bank = psum.tile([P, BANK], F32, tag="bank")
-                for q in range(BANK // P):
-                    j = half * (BANK // P) + q
-                    for path in range(PATHS):
-                        nc.tensor.matmul(
-                            out=bank[:, q * P : (q + 1) * P], lhsT=interf_t[:, path, j, tokens], rhs=ident_f32[:],
-                            is_transpose=True, start=(path == 0), stop=(path == PATHS - 1),
-                        )
-                y_banks[tt].append(bank)
+            for j in range(FEATURE_TILES):
+                quad, k = divmod(j, 4)
+                nc.scalar.activation(
+                    out=interf_t[:, path, j, tokens], in_=memory["t", tt, path, quad][:, k, :], func=ACT.Identity,
+                    scale=mod[:, path, j : j + 1], bias=bias_sum[:, j : j + 1] if path == 0 else 0.0,
+                )
 
-        def add_hn(tt):
-            add_and_sum(tt, x_all[:, tt, :], y_banks[tt], hn_all[:, tt, :])
+        def transpose_y(tt, half):
+            tokens = slice(tt * P, (tt + 1) * P)
+            y_bank = bank("left", [P, BANK], F32, ("centre", tt))
+            memory["y", tt, half] = y_bank
+            for q in range(BANK // P):
+                j = half * (BANK // P) + q
+                terms = [hn_t[:, j, tokens], interf_t[:, 0, j, tokens], interf_t[:, 1, j, tokens]]
+                for n, term in enumerate(terms):
+                    nc.tensor.matmul(
+                        out=y_bank[:, q * P : (q + 1) * P], lhsT=term, rhs=ident_f32[:],
+                        is_transpose=True, start=(n == 0), stop=(n == len(terms) - 1),
+                    )
 
-        def second_norm_centre(tt):
-            statistics(tt, x_all[:, tt, :])
-            centre_and_gain(tt, hn_all[:, tt, :], x_all[:, tt, :], ln4_g_spread)
+        def row_statistics(tt, half):
+            if half == 0:
+                memory["parts", tt] = stats.tile([P, HALVES, 6], F32, name="parts")
+            nc.vector.bn_stats(out=memory["parts", tt][:, half, :], in_=memory["y", tt, half][:])
+            if half == HALVES - 1:
+                memory["mean_var", tt] = stats.tile([P, 2], F32, name="mean_var")
+                nc.vector.bn_aggr(
+                    out=memory["mean_var", tt][:], in_=memory["parts", tt][:].rearrange("p h s -> p (h s)")
+                )
 
-        def second_norm_scale(tt):
+        def second_rstd(tt):
+            memory["rstd2", tt] = stats.tile([P, 1], F32, name="rstd2")
+            nc.scalar.activation(
+                out=memory["rstd2", tt][:], in_=memory["mean_var", tt][:, 1:2], func=ACT.Abs_reciprocal_sqrt,
+                bias=eps[:], scale=1.0,
+            )
+
+        def centre(tt):
             for half in range(HALVES):
                 cols = slice(half * BANK, (half + 1) * BANK)
-                scale_and_shift(tt, hn_all[:, tt, cols], ln4_b_spread[:, cols])
-                nc.sync.dma_start(out=out_rows[tt * P : (tt + 1) * P, cols], in_=hn_all[:, tt, cols])
+                nc.vector.scalar_tensor_tensor(
+                    out=x_all[:, tt, cols], in0=memory["y", tt, half][:], scalar=memory["mean_var", tt][:, 0:1],
+                    in1=ln4_g_spread[:, cols], op0=ALU.subtract, op1=ALU.mult,
+                )
 
-        stages = [
-            add_ent, first_norm_centre, first_norm_scale, transpose_hn, round_hn, quantise_hn, stage2,
-            transpose_interf, add_hn, second_norm_centre, second_norm_scale,
-        ]
-        for r in range(len(stages) + TILE_SKEW * (TOKEN_TILES - 1)):
-            if ENT_PASSES + 1 + r <= len(chunks):
-                weight_step(ENT_PASSES + 1 + r)
-            for tt in reversed(range(TOKEN_TILES)):
-                s = r - TILE_SKEW * tt
-                if 0 <= s < len(stages):
-                    stages[s](tt)
+        def finish(tt):
+            for half in range(HALVES):
+                cols = slice(half * BANK, (half + 1) * BANK)
+                nc.vector.scalar_tensor_tensor(
+                    out=x_all[:, tt, cols], in0=x_all[:, tt, cols], scalar=memory["rstd2", tt][:],
+                    in1=ln4_b_spread[:, cols], op0=ALU.mult, op1=ALU.add,
+                )
+                nc.sync.dma_start(out=out_rows[tt * P : (tt + 1) * P, cols], in_=x_all[:, tt, cols])
+
+        block_of = {b: i for i, b in enumerate(BLOCKS)}
+
+        def task(name, needs, write, banks=None):
+            tasks[name] = (needs, write, banks)
+
+        for i, (kind, index) in enumerate(BLOCKS):
+            before = i - RAW_BUFS
+            freed = []
+            if before >= 0:
+                freed = [("transpose_e", before)] if BLOCKS[before][0] == "e" else [("vcopy", before), ("scopy", before)]
+            task(("load", i), freed, lambda i=i: load(i))
+            reuse = [("quantise", i - GROUPED_BUFS)] if i >= GROUPED_BUFS else []
+            if kind == "e":
+                task(("transpose_e", i), [("load", i)], lambda i=i: transpose_e(i), ("right", 4))
+                task(("empty_e", i), [("transpose_e", i)] + reuse, lambda i=i: empty_e(i))
+                task(("quantise", i), [("empty_e", i)], lambda i=i: quantise(i))
+            else:
+                split = vector_cols(i)
+                task(("vcopy", i), [("load", i)] + reuse, lambda i=i, s=split: regroup(i, nc.vector.tensor_copy, 0, s) if s > 0 else None)
+                task(("scopy", i), [("load", i)] + reuse, lambda i=i, s=split: regroup(i, nc.scalar.copy, s, FEATURES) if s < FEATURES else None)
+                task(("quantise", i), [("vcopy", i), ("scopy", i)], lambda i=i: quantise(i))
+        last_e = max(i for i, b in enumerate(BLOCKS) if b[0] == "e")
+        for tt in range(TOKEN_TILES):
+            task(("load_h", tt), [], lambda tt=tt: load_h(tt))
+            for c in range(ENT_PASSES):
+                needs = [("quantise", block_of["e", tt]), ("quantise", block_of["ent", c])]
+                if tt >= TOKEN_TILES // 2:
+                    needs += [("empty_e", last_e), "copy_ent_pb", "copy_vectors"]
+                task(("multiply", c, tt), needs, lambda c=c, tt=tt: multiply(c, tt),
+                     ("left" if tt < TOKEN_TILES // 2 else "right", 2) if c == 0 else None)
+            task(("start_x", tt), [("load_h", tt), "copy_ent_pb"], lambda tt=tt: start_x(tt))
+            task(("add_ent", tt), [("start_x", tt)] + [("multiply", c, tt) for c in range(ENT_PASSES)], lambda tt=tt: add_ent(tt))
+            task(("mean", tt), [("add_ent", tt)], lambda tt=tt: mean(tt))
+            task(("squares", tt), [("mean", tt)], lambda tt=tt: squares(tt))
+            task(("first_rstd", tt), [("squares", tt)], lambda tt=tt: first_rstd(tt))
+            task(("normalise", tt), [("first_rstd", tt)], lambda tt=tt: normalise(tt))
+            task(("transpose_z", tt), [("normalise", tt)], lambda tt=tt: transpose_z(tt), ("right", 2))
+            task(("gain_shift", tt), [("transpose_z", tt), "copy_vectors"], lambda tt=tt: gain_shift(tt))
+            task(("round_hn", tt), [("gain_shift", tt)], lambda tt=tt: round_hn(tt))
+            task(("quantise_hn", tt), [("round_hn", tt)], lambda tt=tt: quantise_hn(tt))
+            for path in range(PATHS):
+                chunks = [block_of["path", path * PATH_PASSES + c] for c in range(PATH_PASSES)]
+                task(("products", tt, path), [("quantise_hn", tt)] + [("quantise", i) for i in chunks],
+                     lambda tt=tt, path=path: products(tt, path), ("right", 2))
+                task(("weigh", tt, path), [("products", tt, path), ("chore", len(chores) - 1)], lambda tt=tt, path=path: weigh(tt, path))
+            for half in range(HALVES):
+                task(("transpose_y", tt, half), [("weigh", tt, 0), ("weigh", tt, 1)], lambda tt=tt, half=half: transpose_y(tt, half), ("left", 1))
+                task(("row_stats", tt, half), [("transpose_y", tt, half)] + ([("row_stats", tt, 0)] if half else []), lambda tt=tt, half=half: row_statistics(tt, half))
+            task(("second_rstd", tt), [("row_stats", tt, 1)], lambda tt=tt: second_rstd(tt))
+            task(("centre", tt), [("row_stats", tt, 1), "load_ln4"], lambda tt=tt: centre(tt))
+            task(("finish", tt), [("centre", tt), ("second_rstd", tt)], lambda tt=tt: finish(tt))
+        task("sin_table", ["load_vectors"], lambda: nc.scalar.activation(out=table_warm[:], in_=eps[:], func=ACT.Sin))
+        task("load_vectors", [], load_vectors)
+        task("load_ln4", [], load_ln4)
+        task("spread_ent_pb", ["load_vectors"], spread_ent_pb, ("right", 1))
+        task("copy_ent_pb", ["spread_ent_pb"], copy_ent_pb)
+        task("turn_vectors", ["load_vectors"], turn_vectors, ("right", 1))
+        task("copy_vectors", ["turn_vectors"], copy_vectors)
+        for n, chore in enumerate(chores):
+            needs = ["copy_vectors"] if n == 0 else [("chore", n - 1)]
+            if n == SINES_BEHIND + 1:
+                needs.append("sines")
+            task(("chore", n), needs, chore)
+        task("sines", [("chore", SINES_BEHIND)], sines)
+        task("norm_table", ["sines"], lambda: nc.scalar.activation(
+            out=table_warm[:], in_=sin_half[:, 0, 0:1], func=ACT.Abs_reciprocal_sqrt, bias=eps[:], scale=0.0))
+
+
+        def write_down(queues):
+            heads = [0 for q in queues]
+            moved = True
+            while moved:
+                moved = False
+                for k, queue in enumerate(queues):
+                    while heads[k] < len(queue):
+                        needs, write, banks = tasks[queue[heads[k]]]
+                        if not all(n in done for n in needs) or (banks is not None and not banks_free(banks[0], banks[1])):
+                            break
+                        write()
+                        done.add(queue[heads[k]])
+                        heads[k] += 1
+                        moved = True
+            return [q[n:] for q, n in zip(queues, heads)]
+
+        first_path = block_of["path", 0]
+        TILE_ORDER = [2, 3, 0, 1]
+        loads = [("load", 0), ("load_h", 0), ("load_h", 1), ("load", 1), ("load_h", 2), ("load_h", 3)]
+        loads += [("load", i) for i in range(2, len(BLOCKS))] + ["load_ln4"]
+        vector = ["copy_vectors"] + [("chore", n) for n in range(SINES_BEHIND + 1)]
+        vector += [("start_x", 0), ("start_x", 1), ("quantise", 0), ("start_x", 2), ("start_x", 3)]
+        vector += [("quantise", 1), ("quantise", 2)]
+        scalar = ["sin_table", "copy_ent_pb", ("empty_e", 0), "sines", "norm_table"] + [("empty_e", i) for i in range(1, TOKEN_TILES)]
+        tensor = ["spread_ent_pb", "turn_vectors"] + [("transpose_e", i) for i in range(TOKEN_TILES)]
+        first_ent = block_of["ent", 0]
+        for i in range(first_ent, first_path + 1):
+            vector += [("vcopy", i), ("quantise", i - 1)]
+            scalar.append(("scopy", i))
+            n = i - first_ent
+            if SINES_BEHIND + 1 + n < len(chores):
+                vector.append(("chore", SINES_BEHIND + 1 + n))
+            if n >= 1:
+                tensor += [("multiply", n - 1, tt) for tt in TILE_ORDER]
+
+        with tc.tile_pool(name="stage1", bufs=1) as stage1:
+            e_codes = stage1.tile([P, TOKEN_TILES, ENT_PASSES, P], U32, align_bytes=64)
+            e_scales = stage1.tile([P, TOKEN_TILES, ENT_PASSES, P], U8, align_bytes=64)
+            w1_codes = stage1.tile([P, ENT_PASSES, FEATURES], U32, align_bytes=64)
+            w1_scales = stage1.tile([P, ENT_PASSES, FEATURES], U8, align_bytes=64)
+            left = write_down([loads, ["load_vectors"], vector, scalar, tensor])
+        assert not any(left), left
+        tail = ctx.enter_context(tc.tile_pool(name="tail", bufs=1))
+        interf_t = tail.tile([P, PATHS, FEATURE_TILES, TOKENS], F32)
+
+        def of(stage, n, *rest):
+            return [(stage, TILE_ORDER[n]) + rest] if 0 <= n < TOKEN_TILES else []
+
+        vector, scalar, tensor = [], [], of("transpose_z", 0) + of("transpose_z", 1)
+        for n in range(TOKEN_TILES):
+            chunk = first_path + n
+            if chunk + 1 < len(BLOCKS):
+                vector.append(("vcopy", chunk + 1))
+                scalar.append(("scopy", chunk + 1))
+            else:
+                scalar += of("weigh", 0, 0)
+            vector += of("add_ent", n) + [("quantise", chunk)] + of("normalise", n - 1)
+            vector += of("round_hn", n - 2) + of("quantise_hn", n - 2)
+            scalar += of("mean", n) + of("squares", n)
+            scalar += of("gain_shift", n - 1) if n < TOKEN_TILES - 1 else of("weigh", 0, 1)
+            scalar += of("first_rstd", n)
+        vector += of("normalise", TOKEN_TILES - 1)
+        for n in range(TOKEN_TILES):
+            tensor += of("products", n, 0) + of("products", n, 1) + of("transpose_z", n + 2)
+            tensor += of("transpose_y", n, 0) + of("transpose_y", n, 1)
+            scalar += of("gain_shift", n + 2) + of("weigh", n + 1, 0) + of("second_rstd", n) + of("weigh", n + 1, 1)
+            vector += of("row_stats", n, 0) + of("row_stats", n, 1) + of("centre", n)
+            vector += of("round_hn", n + 2) + of("quantise_hn", n + 2) + of("finish", n)
+
+        left = write_down([vector, scalar, tensor])
+        assert not any(left), left

@@ -369,11 +369,10 @@ def tile_quantuminspiredneuralcore_pb_kernel(
             if half == 0:
                 memory["parts", tt] = stats.tile([P, HALVES, 6], F32, name="parts")
             nc.vector.bn_stats(out=memory["parts", tt][:, half, :], in_=memory["y", tt, half][:])
-            if half == HALVES - 1:
-                memory["mean_var", tt] = stats.tile([P, 2], F32, name="mean_var")
-                nc.vector.bn_aggr(
-                    out=memory["mean_var", tt][:], in_=memory["parts", tt][:].rearrange("p h s -> p (h s)")
-                )
+
+        def aggregate(tt):
+            memory["mean_var", tt] = stats.tile([P, 2], F32, name="mean_var")
+            nc.vector.bn_aggr(out=memory["mean_var", tt][:], in_=memory["parts", tt][:].rearrange("p h s -> p (h s)"))
 
         def second_rstd(tt):
             memory["rstd2", tt] = stats.tile([P, 1], F32, name="rstd2")
@@ -447,8 +446,9 @@ def tile_quantuminspiredneuralcore_pb_kernel(
             for half in range(HALVES):
                 task(("transpose_y", tt, half), [("weigh", tt, 0), ("weigh", tt, 1)], lambda tt=tt, half=half: transpose_y(tt, half), ("left", 1))
                 task(("row_stats", tt, half), [("transpose_y", tt, half)] + ([("row_stats", tt, 0)] if half else []), lambda tt=tt, half=half: row_statistics(tt, half))
-            task(("second_rstd", tt), [("row_stats", tt, 1)], lambda tt=tt: second_rstd(tt))
-            task(("centre", tt), [("row_stats", tt, 1), "load_ln4"], lambda tt=tt: centre(tt))
+            task(("aggregate", tt), [("row_stats", tt, 0), ("row_stats", tt, 1)], lambda tt=tt: aggregate(tt))
+            task(("second_rstd", tt), [("aggregate", tt)], lambda tt=tt: second_rstd(tt))
+            task(("centre", tt), [("aggregate", tt), "load_ln4"], lambda tt=tt: centre(tt))
             task(("finish", tt), [("centre", tt), ("second_rstd", tt)], lambda tt=tt: finish(tt))
         task("sin_table", ["load_vectors"], lambda: nc.scalar.activation(out=table_warm[:], in_=eps[:], func=ACT.Sin))
         task("load_vectors", [], load_vectors)
@@ -515,26 +515,27 @@ def tile_quantuminspiredneuralcore_pb_kernel(
         def of(stage, n, *rest):
             return [(stage, TILE_ORDER[n]) + rest] if 0 <= n < TOKEN_TILES else []
 
-        vector, scalar, tensor = [], [], of("transpose_z", 0) + of("transpose_z", 1)
+        def chunk(stage, n):
+            return [(stage, first_path + n)]
+
+        vector = chunk("vcopy", 1) + of("add_ent", 0) + of("add_ent", 1) + chunk("quantise", 0) + of("normalise", 0)
+        vector += chunk("vcopy", 2) + of("add_ent", 2) + of("normalise", 1) + chunk("quantise", 1) + of("round_hn", 0)
+        vector += chunk("vcopy", 3) + of("quantise_hn", 0) + chunk("quantise", 2) + chunk("quantise", 3)
+        vector += of("normalise", 2) + of("add_ent", 3) + of("round_hn", 1) + of("quantise_hn", 1) + of("normalise", 3)
+        scalar = chunk("scopy", 1) + of("mean", 0) + of("squares", 0) + of("mean", 1) + of("first_rstd", 0) + of("squares", 1)
+        scalar += chunk("scopy", 2) + of("first_rstd", 1) + of("gain_shift", 0) + of("mean", 2)
+        scalar += chunk("scopy", 3) + of("squares", 2) + of("gain_shift", 1) + of("first_rstd", 2)
+        scalar += of("weigh", 0, 0) + of("weigh", 0, 1)
+        scalar += of("mean", 3) + of("gain_shift", 2) + of("squares", 3) + of("first_rstd", 3)
+        tensor = of("transpose_z", 0) + of("transpose_z", 1) + of("products", 0, 0) + of("products", 0, 1)
         for n in range(TOKEN_TILES):
-            chunk = first_path + n
-            if chunk + 1 < len(BLOCKS):
-                vector.append(("vcopy", chunk + 1))
-                scalar.append(("scopy", chunk + 1))
-            else:
-                scalar += of("weigh", 0, 0)
-            vector += of("add_ent", n) + [("quantise", chunk)] + of("normalise", n - 1)
-            vector += of("round_hn", n - 2) + of("quantise_hn", n - 2)
-            scalar += of("mean", n) + of("squares", n)
-            scalar += of("gain_shift", n - 1) if n < TOKEN_TILES - 1 else of("weigh", 0, 1)
-            scalar += of("first_rstd", n)
-        vector += of("normalise", TOKEN_TILES - 1)
-        for n in range(TOKEN_TILES):
-            tensor += of("products", n, 0) + of("products", n, 1) + of("transpose_z", n + 2)
-            tensor += of("transpose_y", n, 0) + of("transpose_y", n, 1)
-            scalar += of("gain_shift", n + 2) + of("weigh", n + 1, 0) + of("second_rstd", n) + of("weigh", n + 1, 1)
-            vector += of("row_stats", n, 0) + of("row_stats", n, 1) + of("centre", n)
-            vector += of("round_hn", n + 2) + of("quantise_hn", n + 2) + of("finish", n)
+            tensor += of("transpose_z", n + 2)
+            for half in range(HALVES):
+                tensor += of("transpose_y", n, half) + of("products", n + 1, half)
+            scalar += of("weigh", n + 1, 0) + of("weigh", n + 1, 1) + of("second_rstd", n) + of("gain_shift", n + 3)
+            vector += of("row_stats", n, 0) + of("round_hn", n + 2) + of("quantise_hn", n + 2) + of("row_stats", n, 1)
+            vector += of("finish", n - 1) + of("aggregate", n) + of("centre", n)
+        vector += of("finish", TOKEN_TILES - 1)
 
         left = write_down([vector, scalar, tensor])
         assert not any(left), left

@@ -39,8 +39,6 @@ GROUPED_BUFS = 3
 ENT_VECTOR_COLS = 480
 PATH_VECTOR_COLS = 512
 
-TWO_PI_HEAD = 6.28125
-TWO_PI_REST = 2.0 * math.pi - TWO_PI_HEAD
 ROUND_TO_INT = 12582912.0
 
 FLOPS = 2 * TOKENS * K_ENT * FEATURES + 2 * PATHS * TOKENS * FEATURES * FEATURES
@@ -72,6 +70,8 @@ def tile_quantuminspiredneuralcore_pb_kernel(
         nc.vector.memset(ent_pb_rows[:].bitcast(I32), 0)
         vec_rows = consts.tile([P, FEATURES], BF16)
         nc.vector.memset(vec_rows[:].bitcast(I32), 0)
+        ln3_rows = consts.tile([P, FEATURES], BF16)
+        nc.vector.memset(ln3_rows[:].bitcast(I32), 0)
         ident_bf16 = consts.tile([P, P], BF16)
         nc.vector.tensor_copy(out=ident_bf16[:], in_=ident_f32[:])
         table_warm = consts.tile([P, 1], F32)
@@ -87,10 +87,10 @@ def tile_quantuminspiredneuralcore_pb_kernel(
         ln4_g_spread = consts.tile([P, FEATURES], BF16)
         ln4_b_spread = consts.tile([P, FEATURES], BF16)
         ent_pb_spread = consts.tile([P, FEATURES], BF16)
-        VECS = 6
-        vec_cols = consts.tile([P, VECS, FEATURE_TILES], F32)
-        ln3_g_cols, ln3_b_cols = vec_cols[:, 0, :], vec_cols[:, 1, :]
-        path_b_cols, phase_cols = vec_cols[:, 2:4, :], vec_cols[:, 4:6, :]
+        vec_cols = consts.tile([P, 2 * PATHS, FEATURE_TILES], F32)
+        path_b_cols, phase_cols = vec_cols[:, 0:PATHS, :], vec_cols[:, PATHS : 2 * PATHS, :]
+        ln3_cols = consts.tile([P, 2, FEATURE_TILES], F32)
+        ln3_g_cols, ln3_b_cols = ln3_cols[:, 0, :], ln3_cols[:, 1, :]
         turns = consts.tile([P, PATHS, FEATURE_TILES], F32)
         angle = consts.tile([P, PATHS, FEATURE_TILES], F32)
         sin_full = consts.tile([P, PATHS, FEATURE_TILES], F32)
@@ -126,19 +126,24 @@ def tile_quantuminspiredneuralcore_pb_kernel(
                 for part in range(parts):
                     cols = slice(part * (K_ENT // parts), (part + 1) * (K_ENT // parts))
                     nc.sync.dma_start(out=raw[i][:, cols], in_=e_rows[index * P : (index + 1) * P, cols])
+                    if index == 0 and part == 0:
+                        load_vectors()
             else:
                 rows = weight_rows(kind, index)
                 nc.sync.dma_start(out=raw[i][:].rearrange("p (a b) -> p a b", a=rows.shape[1]), in_=rows)
 
         def load_h(tt):
-            nc.sync.dma_start(out=h_sb[:, tt, :], in_=h_rows[tt * P : (tt + 1) * P, :])
+            rows = h_rows[tt * P : (tt + 2) * P, :].rearrange("(t p) f -> p t f", p=P)
+            nc.sync.dma_start(out=h_sb[:, tt : tt + 2, :], in_=rows)
 
         def load_vectors():
-            nc.scalar.dma_start(out=ent_pb_rows[0:1, :], in_=ent_pb.unsqueeze(0))
-            nc.scalar.dma_start(out=vec_rows[0:1, :], in_=ln3_g.unsqueeze(0))
-            nc.scalar.dma_start(out=vec_rows[1:2, :], in_=ln3_b.unsqueeze(0))
-            nc.scalar.dma_start(out=vec_rows[2:4, :], in_=path_b)
-            nc.scalar.dma_start(out=vec_rows[4:6, :], in_=phase)
+            nc.sync.dma_start(out=ent_pb_rows[0:1, :], in_=ent_pb.unsqueeze(0))
+            nc.sync.dma_start(out=vec_rows[PATHS : 2 * PATHS, :], in_=phase)
+            nc.sync.dma_start(out=vec_rows[0:PATHS, :], in_=path_b)
+
+        def load_ln3():
+            nc.sync.dma_start(out=ln3_rows[0:1, :], in_=ln3_g.unsqueeze(0))
+            nc.sync.dma_start(out=ln3_rows[1:2, :], in_=ln3_b.unsqueeze(0))
 
         def load_ln4():
             nc.sync.dma_start(out=ln4_g_spread[:], in_=ln4_g.partition_broadcast(P))
@@ -149,22 +154,23 @@ def tile_quantuminspiredneuralcore_pb_kernel(
                 grouped[i] = grouped_pool.tile([P, K_ENT], BF16, tag="grouped", name="grouped", align_bytes=64)
             return grouped[i]
 
-        def transpose_e(i):
+        def transpose_e(i, half):
             e_words = raw[i][:].bitcast(F32)
-            memory["e", i] = []
-            for pair in range(ENT_PASSES // 2):
-                e_bank = bank("right", [P, 2, 2, P], F32, ("empty_e", i))
+            for pair in (2 * half, 2 * half + 1):
+                e_bank = bank("right", [P, 2, 2, P], F32, ("empty_e", i, half))
                 for c2 in range(2):
                     for u in range(2):
                         first = (2 * pair + c2) * 2 * P + u * P
                         nc.tensor.transpose(e_bank[:, c2, u, :], e_words[:, first : first + P], ident_f32[:])
-                memory["e", i].append(e_bank)
+                memory["e", i, pair] = e_bank
 
-        def empty_e(i):
+        def empty_e(i, half):
             grouped_words = grouped_tile(i)[:].bitcast(F32).rearrange("p (c r u) -> p c r u", c=ENT_PASSES, u=2)
-            for pair, e_bank in enumerate(memory["e", i]):
-                nc.scalar.copy(
-                    out=grouped_words[:, 2 * pair : 2 * pair + 2], in_=e_bank[:].rearrange("p c u r -> p c r u")
+            for pair in (2 * half, 2 * half + 1):
+                copy = nc.vector.tensor_copy if (i, half) == (0, 0) else nc.scalar.copy
+                copy(
+                    out=grouped_words[:, 2 * pair : 2 * pair + 2],
+                    in_=memory["e", i, pair][:].rearrange("p c u r -> p c r u"),
                 )
 
         def regroup(i, copy, first, last):
@@ -222,7 +228,15 @@ def tile_quantuminspiredneuralcore_pb_kernel(
                 nc.tensor.transpose(memory["cols"][:, j, :], vec_rows[:, j * P : (j + 1) * P], ident_bf16[:])
 
         def copy_vectors():
-            nc.vector.tensor_copy(out=vec_cols[:], in_=memory["cols"][:, :, 0:VECS].rearrange("p j r -> p r j"))
+            nc.vector.tensor_copy(out=vec_cols[:], in_=memory["cols"][:, :, 0 : 2 * PATHS].rearrange("p j r -> p r j"))
+
+        def turn_ln3():
+            memory["ln3"] = bank("right", [P, FEATURE_TILES, P], BF16, "copy_ln3")
+            for j in range(FEATURE_TILES):
+                nc.tensor.transpose(memory["ln3"][:, j, :], ln3_rows[:, j * P : (j + 1) * P], ident_bf16[:])
+
+        def copy_ln3():
+            nc.vector.tensor_copy(out=ln3_cols[:], in_=memory["ln3"][:, :, 0:2].rearrange("p j r -> p r j"))
 
         def sines():
             nc.scalar.activation(out=sin_full[:], in_=angle[:], func=ACT.Sin)
@@ -237,10 +251,7 @@ def tile_quantuminspiredneuralcore_pb_kernel(
                 out=turns[:], in0=turns[:], scalar1=ROUND_TO_INT, scalar2=None, op0=ALU.subtract
             ),
             lambda: nc.vector.scalar_tensor_tensor(
-                out=angle[:], in0=turns[:], scalar=-TWO_PI_HEAD, in1=phase_cols, op0=ALU.mult, op1=ALU.add
-            ),
-            lambda: nc.vector.scalar_tensor_tensor(
-                out=angle[:], in0=turns[:], scalar=-TWO_PI_REST, in1=angle[:], op0=ALU.mult, op1=ALU.add
+                out=angle[:], in0=turns[:], scalar=-2.0 * math.pi, in1=phase_cols, op0=ALU.mult, op1=ALU.add
             ),
             lambda: nc.vector.tensor_tensor(out=mod[:], in0=sin_half[:], in1=sin_half[:], op=ALU.mult),
             lambda: nc.vector.tensor_scalar(
@@ -250,7 +261,7 @@ def tile_quantuminspiredneuralcore_pb_kernel(
             lambda: nc.vector.tensor_tensor(out=bias_mod[:], in0=path_b_cols, in1=mod[:], op=ALU.mult),
             lambda: nc.vector.tensor_tensor(out=bias_sum[:], in0=bias_mod[:, 0, :], in1=bias_mod[:, 1, :], op=ALU.add),
         ]
-        SINES_BEHIND = 3
+        SINES_BEHIND = 2
 
         def start_x(tt):
             nc.vector.tensor_tensor(out=x_all[:, tt, :], in0=h_sb[:, tt, :], in1=ent_pb_spread[:], op=ALU.add)
@@ -352,13 +363,21 @@ def tile_quantuminspiredneuralcore_pb_kernel(
                     scale=mod[:, path, j : j + 1], bias=bias_sum[:, j : j + 1] if path == 0 else 0.0,
                 )
 
+        def add_hn(tt, half):
+            tokens = slice(tt * P, (tt + 1) * P)
+            for j in range(half * (FEATURE_TILES // 2), (half + 1) * (FEATURE_TILES // 2), 2):
+                nc.gpsimd.tensor_tensor(
+                    out=interf_t[:, 0, j : j + 2, tokens], in0=interf_t[:, 0, j : j + 2, tokens],
+                    in1=hn_t[:, j : j + 2, tokens], op=ALU.add,
+                )
+
         def transpose_y(tt, half):
             tokens = slice(tt * P, (tt + 1) * P)
             y_bank = bank("left", [P, BANK], F32, ("centre", tt))
             memory["y", tt, half] = y_bank
             for q in range(BANK // P):
                 j = half * (BANK // P) + q
-                terms = [hn_t[:, j, tokens], interf_t[:, 0, j, tokens], interf_t[:, 1, j, tokens]]
+                terms = [interf_t[:, 0, j, tokens], interf_t[:, 1, j, tokens]]
                 for n, term in enumerate(terms):
                     nc.tensor.matmul(
                         out=y_bank[:, q * P : (q + 1) * P], lhsT=term, rhs=ident_f32[:],
@@ -407,13 +426,14 @@ def tile_quantuminspiredneuralcore_pb_kernel(
             before = i - RAW_BUFS
             freed = []
             if before >= 0:
-                freed = [("transpose_e", before)] if BLOCKS[before][0] == "e" else [("vcopy", before), ("scopy", before)]
+                freed = [("transpose_e", before, 0), ("transpose_e", before, 1)] if BLOCKS[before][0] == "e" else [("vcopy", before), ("scopy", before)]
             task(("load", i), freed, lambda i=i: load(i))
             reuse = [("quantise", i - GROUPED_BUFS)] if i >= GROUPED_BUFS else []
             if kind == "e":
-                task(("transpose_e", i), [("load", i)], lambda i=i: transpose_e(i), ("right", 4))
-                task(("empty_e", i), [("transpose_e", i)] + reuse, lambda i=i: empty_e(i))
-                task(("quantise", i), [("empty_e", i)], lambda i=i: quantise(i))
+                for half in range(2):
+                    task(("transpose_e", i, half), [("load", i)], lambda i=i, half=half: transpose_e(i, half), ("right", 2))
+                    task(("empty_e", i, half), [("transpose_e", i, half)] + reuse, lambda i=i, half=half: empty_e(i, half))
+                task(("quantise", i), [("empty_e", i, 0), ("empty_e", i, 1)], lambda i=i: quantise(i))
             else:
                 split = vector_cols(i)
                 task(("vcopy", i), [("load", i)] + reuse, lambda i=i, s=split: regroup(i, nc.vector.tensor_copy, 0, s) if s > 0 else None)
@@ -421,21 +441,22 @@ def tile_quantuminspiredneuralcore_pb_kernel(
                 task(("quantise", i), [("vcopy", i), ("scopy", i)], lambda i=i: quantise(i))
         last_e = max(i for i, b in enumerate(BLOCKS) if b[0] == "e")
         for tt in range(TOKEN_TILES):
-            task(("load_h", tt), [], lambda tt=tt: load_h(tt))
+            if tt % 2 == 0:
+                task(("load_h", tt), [], lambda tt=tt: load_h(tt))
             for c in range(ENT_PASSES):
                 needs = [("quantise", block_of["e", tt]), ("quantise", block_of["ent", c])]
                 if tt >= TOKEN_TILES // 2:
-                    needs += [("empty_e", last_e), "copy_ent_pb", "copy_vectors"]
+                    needs += [("empty_e", last_e, 1), "copy_ent_pb", "copy_vectors", "copy_ln3"]
                 task(("multiply", c, tt), needs, lambda c=c, tt=tt: multiply(c, tt),
                      ("left" if tt < TOKEN_TILES // 2 else "right", 2) if c == 0 else None)
-            task(("start_x", tt), [("load_h", tt), "copy_ent_pb"], lambda tt=tt: start_x(tt))
+            task(("start_x", tt), [("load_h", tt - tt % 2), "copy_ent_pb"], lambda tt=tt: start_x(tt))
             task(("add_ent", tt), [("start_x", tt)] + [("multiply", c, tt) for c in range(ENT_PASSES)], lambda tt=tt: add_ent(tt))
             task(("mean", tt), [("add_ent", tt)], lambda tt=tt: mean(tt))
             task(("squares", tt), [("mean", tt)], lambda tt=tt: squares(tt))
             task(("first_rstd", tt), [("squares", tt)], lambda tt=tt: first_rstd(tt))
             task(("normalise", tt), [("first_rstd", tt)], lambda tt=tt: normalise(tt))
             task(("transpose_z", tt), [("normalise", tt)], lambda tt=tt: transpose_z(tt), ("right", 2))
-            task(("gain_shift", tt), [("transpose_z", tt), "copy_vectors"], lambda tt=tt: gain_shift(tt))
+            task(("gain_shift", tt), [("transpose_z", tt), "copy_ln3"], lambda tt=tt: gain_shift(tt))
             task(("round_hn", tt), [("gain_shift", tt)], lambda tt=tt: round_hn(tt))
             task(("quantise_hn", tt), [("round_hn", tt)], lambda tt=tt: quantise_hn(tt))
             for path in range(PATHS):
@@ -444,19 +465,22 @@ def tile_quantuminspiredneuralcore_pb_kernel(
                      lambda tt=tt, path=path: products(tt, path), ("right", 2))
                 task(("weigh", tt, path), [("products", tt, path), ("chore", len(chores) - 1)], lambda tt=tt, path=path: weigh(tt, path))
             for half in range(HALVES):
-                task(("transpose_y", tt, half), [("weigh", tt, 0), ("weigh", tt, 1)], lambda tt=tt, half=half: transpose_y(tt, half), ("left", 1))
+                task(("add_hn", tt, half), [("weigh", tt, 0)], lambda tt=tt, half=half: add_hn(tt, half))
+                task(("transpose_y", tt, half), [("add_hn", tt, half), ("weigh", tt, 1)], lambda tt=tt, half=half: transpose_y(tt, half), ("left", 1))
                 task(("row_stats", tt, half), [("transpose_y", tt, half)] + ([("row_stats", tt, 0)] if half else []), lambda tt=tt, half=half: row_statistics(tt, half))
             task(("aggregate", tt), [("row_stats", tt, 0), ("row_stats", tt, 1)], lambda tt=tt: aggregate(tt))
             task(("second_rstd", tt), [("aggregate", tt)], lambda tt=tt: second_rstd(tt))
             task(("centre", tt), [("aggregate", tt), "load_ln4"], lambda tt=tt: centre(tt))
             task(("finish", tt), [("centre", tt), ("second_rstd", tt)], lambda tt=tt: finish(tt))
-        task("sin_table", ["load_vectors"], lambda: nc.scalar.activation(out=table_warm[:], in_=eps[:], func=ACT.Sin))
-        task("load_vectors", [], load_vectors)
+        task("sin_table", [], lambda: nc.scalar.activation(out=table_warm[:], in_=eps[:], func=ACT.Sin))
         task("load_ln4", [], load_ln4)
-        task("spread_ent_pb", ["load_vectors"], spread_ent_pb, ("right", 1))
+        task("spread_ent_pb", [("load", 0)], spread_ent_pb, ("right", 1))
         task("copy_ent_pb", ["spread_ent_pb"], copy_ent_pb)
-        task("turn_vectors", ["load_vectors"], turn_vectors, ("right", 1))
+        task("turn_vectors", [("load", 0)], turn_vectors, ("right", 1))
         task("copy_vectors", ["turn_vectors"], copy_vectors)
+        task("load_ln3", [], load_ln3)
+        task("turn_ln3", ["load_ln3"], turn_ln3, ("right", 1))
+        task("copy_ln3", ["turn_ln3"], copy_ln3)
         for n, chore in enumerate(chores):
             needs = ["copy_vectors"] if n == 0 else [("chore", n - 1)]
             if n == SINES_BEHIND + 1:
@@ -485,13 +509,17 @@ def tile_quantuminspiredneuralcore_pb_kernel(
 
         first_path = block_of["path", 0]
         TILE_ORDER = [2, 3, 0, 1]
-        loads = [("load", 0), ("load_h", 0), ("load_h", 1), ("load", 1), ("load_h", 2), ("load_h", 3)]
-        loads += [("load", i) for i in range(2, len(BLOCKS))] + ["load_ln4"]
+        loads = [("load", 0), ("load_h", 0), ("load", 1), ("load_h", 2), ("load", 2), "load_ln3"]
+        loads += [("load", i) for i in range(3, len(BLOCKS))] + ["load_ln4"]
         vector = ["copy_vectors"] + [("chore", n) for n in range(SINES_BEHIND + 1)]
-        vector += [("start_x", 0), ("start_x", 1), ("quantise", 0), ("start_x", 2), ("start_x", 3)]
-        vector += [("quantise", 1), ("quantise", 2)]
-        scalar = ["sin_table", "copy_ent_pb", ("empty_e", 0), "sines", "norm_table"] + [("empty_e", i) for i in range(1, TOKEN_TILES)]
-        tensor = ["spread_ent_pb", "turn_vectors"] + [("transpose_e", i) for i in range(TOKEN_TILES)]
+        vector += [("empty_e", 0, 0), ("start_x", 0), ("start_x", 1), ("quantise", 0), ("start_x", 2), ("start_x", 3), ("quantise", 1), ("quantise", 2), "copy_ln3"]
+        scalar = ["sin_table", "copy_ent_pb"]
+        for i in range(TOKEN_TILES):
+            scalar += [("empty_e", i, half) for half in range(2) if (i, half) != (0, 0)]
+            if i == 0:
+                scalar += ["sines", "norm_table"]
+        tensor = ["spread_ent_pb", "turn_vectors", ("transpose_e", 0, 0), ("transpose_e", 0, 1)]
+        tensor += [("transpose_e", i, half) for i in range(1, TOKEN_TILES) for half in range(2)] + ["turn_ln3"]
         first_ent = block_of["ent", 0]
         for i in range(first_ent, first_path + 1):
             vector += [("vcopy", i), ("quantise", i - 1)]
@@ -507,7 +535,7 @@ def tile_quantuminspiredneuralcore_pb_kernel(
             e_scales = stage1.tile([P, TOKEN_TILES, ENT_PASSES, P], U8, align_bytes=64)
             w1_codes = stage1.tile([P, ENT_PASSES, FEATURES], U32, align_bytes=64)
             w1_scales = stage1.tile([P, ENT_PASSES, FEATURES], U8, align_bytes=64)
-            left = write_down([loads, ["load_vectors"], vector, scalar, tensor])
+            left = write_down([loads, vector, scalar, tensor])
         assert not any(left), left
         tail = ctx.enter_context(tc.tile_pool(name="tail", bufs=1))
         interf_t = tail.tile([P, PATHS, FEATURE_TILES, TOKENS], F32)
@@ -536,6 +564,7 @@ def tile_quantuminspiredneuralcore_pb_kernel(
             vector += of("row_stats", n, 0) + of("round_hn", n + 2) + of("quantise_hn", n + 2) + of("row_stats", n, 1)
             vector += of("finish", n - 1) + of("aggregate", n) + of("centre", n)
         vector += of("finish", TOKEN_TILES - 1)
+        gpsimd = [("add_hn", tt, half) for tt in TILE_ORDER for half in range(HALVES)]
 
-        left = write_down([vector, scalar, tensor])
+        left = write_down([vector, scalar, tensor, gpsimd])
         assert not any(left), left

@@ -363,21 +363,13 @@ def tile_quantuminspiredneuralcore_pb_kernel(
                     scale=mod[:, path, j : j + 1], bias=bias_sum[:, j : j + 1] if path == 0 else 0.0,
                 )
 
-        def add_hn(tt, half):
-            tokens = slice(tt * P, (tt + 1) * P)
-            for j in range(half * (FEATURE_TILES // 2), (half + 1) * (FEATURE_TILES // 2), 2):
-                nc.gpsimd.tensor_tensor(
-                    out=interf_t[:, 0, j : j + 2, tokens], in0=interf_t[:, 0, j : j + 2, tokens],
-                    in1=hn_t[:, j : j + 2, tokens], op=ALU.add,
-                )
-
         def transpose_y(tt, half):
             tokens = slice(tt * P, (tt + 1) * P)
             y_bank = bank("left", [P, BANK], F32, ("centre", tt))
             memory["y", tt, half] = y_bank
             for q in range(BANK // P):
                 j = half * (BANK // P) + q
-                terms = [interf_t[:, 0, j, tokens], interf_t[:, 1, j, tokens]]
+                terms = [hn_t[:, j, tokens], interf_t[:, 0, j, tokens], interf_t[:, 1, j, tokens]]
                 for n, term in enumerate(terms):
                     nc.tensor.matmul(
                         out=y_bank[:, q * P : (q + 1) * P], lhsT=term, rhs=ident_f32[:],
@@ -465,8 +457,7 @@ def tile_quantuminspiredneuralcore_pb_kernel(
                      lambda tt=tt, path=path: products(tt, path), ("right", 2))
                 task(("weigh", tt, path), [("products", tt, path), ("chore", len(chores) - 1)], lambda tt=tt, path=path: weigh(tt, path))
             for half in range(HALVES):
-                task(("add_hn", tt, half), [("weigh", tt, 0)], lambda tt=tt, half=half: add_hn(tt, half))
-                task(("transpose_y", tt, half), [("add_hn", tt, half), ("weigh", tt, 1)], lambda tt=tt, half=half: transpose_y(tt, half), ("left", 1))
+                task(("transpose_y", tt, half), [("weigh", tt, 0), ("weigh", tt, 1)], lambda tt=tt, half=half: transpose_y(tt, half), ("left", 1))
                 task(("row_stats", tt, half), [("transpose_y", tt, half)] + ([("row_stats", tt, 0)] if half else []), lambda tt=tt, half=half: row_statistics(tt, half))
             task(("aggregate", tt), [("row_stats", tt, 0), ("row_stats", tt, 1)], lambda tt=tt: aggregate(tt))
             task(("second_rstd", tt), [("aggregate", tt)], lambda tt=tt: second_rstd(tt))
@@ -509,17 +500,18 @@ def tile_quantuminspiredneuralcore_pb_kernel(
 
         first_path = block_of["path", 0]
         TILE_ORDER = [2, 3, 0, 1]
-        loads = [("load", 0), ("load_h", 0), ("load", 1), ("load_h", 2), ("load", 2), "load_ln3"]
+        loads = [("load", 0), ("load_h", 0), ("load", 1), "load_ln3", ("load_h", 2), ("load", 2)]
         loads += [("load", i) for i in range(3, len(BLOCKS))] + ["load_ln4"]
         vector = ["copy_vectors"] + [("chore", n) for n in range(SINES_BEHIND + 1)]
-        vector += [("empty_e", 0, 0), ("start_x", 0), ("start_x", 1), ("quantise", 0), ("start_x", 2), ("start_x", 3), ("quantise", 1), ("quantise", 2), "copy_ln3"]
+        vector += [("empty_e", 0, 0), ("start_x", 0), ("start_x", 1), ("quantise", 0), ("start_x", 2), ("start_x", 3), ("quantise", 1), "copy_ln3", ("quantise", 2)]
         scalar = ["sin_table", "copy_ent_pb"]
         for i in range(TOKEN_TILES):
             scalar += [("empty_e", i, half) for half in range(2) if (i, half) != (0, 0)]
             if i == 0:
                 scalar += ["sines", "norm_table"]
         tensor = ["spread_ent_pb", "turn_vectors", ("transpose_e", 0, 0), ("transpose_e", 0, 1)]
-        tensor += [("transpose_e", i, half) for i in range(1, TOKEN_TILES) for half in range(2)] + ["turn_ln3"]
+        tensor += [("transpose_e", 1, 0), ("transpose_e", 1, 1), "turn_ln3"]
+        tensor += [("transpose_e", i, half) for i in range(2, TOKEN_TILES) for half in range(2)]
         first_ent = block_of["ent", 0]
         for i in range(first_ent, first_path + 1):
             vector += [("vcopy", i), ("quantise", i - 1)]
@@ -564,7 +556,6 @@ def tile_quantuminspiredneuralcore_pb_kernel(
             vector += of("row_stats", n, 0) + of("round_hn", n + 2) + of("quantise_hn", n + 2) + of("row_stats", n, 1)
             vector += of("finish", n - 1) + of("aggregate", n) + of("centre", n)
         vector += of("finish", TOKEN_TILES - 1)
-        gpsimd = [("add_hn", tt, half) for tt in TILE_ORDER for half in range(HALVES)]
 
-        left = write_down([vector, scalar, tensor, gpsimd])
+        left = write_down([vector, scalar, tensor])
         assert not any(left), left

@@ -37,7 +37,7 @@ RAW_BUFS = 6
 GROUPED_BUFS = 3
 
 ENT_VECTOR_COLS = 480
-PATH_VECTOR_COLS = 512
+PATH_VECTOR_COLS = 576
 
 ROUND_TO_INT = 12582912.0
 
@@ -150,8 +150,8 @@ def tile_quantuminspiredneuralcore_pb_kernel(
             nc.sync.dma_start(out=ln4_b_spread[:], in_=ln4_b.partition_broadcast(P))
 
         def grouped_tile(i):
-            if i not in grouped:
-                grouped[i] = grouped_pool.tile([P, K_ENT], BF16, tag="grouped", name="grouped", align_bytes=64)
+            for k in range(len(grouped), i + 1):
+                grouped[k] = grouped_pool.tile([P, K_ENT], BF16, tag="grouped", name="grouped", align_bytes=64)
             return grouped[i]
 
         def transpose_e(i, half):
@@ -503,7 +503,7 @@ def tile_quantuminspiredneuralcore_pb_kernel(
         loads = [("load", 0), ("load_h", 0), ("load", 1), "load_ln3", ("load_h", 2), ("load", 2)]
         loads += [("load", i) for i in range(3, len(BLOCKS))] + ["load_ln4"]
         vector = ["copy_vectors"] + [("chore", n) for n in range(SINES_BEHIND + 1)]
-        vector += [("empty_e", 0, 0), ("start_x", 0), ("start_x", 1), ("quantise", 0), ("start_x", 2), ("start_x", 3), ("quantise", 1), "copy_ln3", ("quantise", 2)]
+        vector += [("empty_e", 0, 0), ("start_x", 0), ("start_x", 1), ("quantise", 0), "copy_ln3", ("start_x", 2), ("start_x", 3), ("quantise", 1), ("quantise", 2)]
         scalar = ["sin_table", "copy_ent_pb"]
         for i in range(TOKEN_TILES):
             scalar += [("empty_e", i, half) for half in range(2) if (i, half) != (0, 0)]
@@ -543,7 +543,7 @@ def tile_quantuminspiredneuralcore_pb_kernel(
         vector += chunk("vcopy", 3) + of("quantise_hn", 0) + chunk("quantise", 2) + chunk("quantise", 3)
         vector += of("normalise", 2) + of("add_ent", 3) + of("round_hn", 1) + of("quantise_hn", 1) + of("normalise", 3)
         scalar = chunk("scopy", 1) + of("mean", 0) + of("squares", 0) + of("mean", 1) + of("first_rstd", 0) + of("squares", 1)
-        scalar += chunk("scopy", 2) + of("first_rstd", 1) + of("gain_shift", 0) + of("mean", 2)
+        scalar += of("first_rstd", 1) + chunk("scopy", 2) + of("gain_shift", 0) + of("mean", 2)
         scalar += chunk("scopy", 3) + of("squares", 2) + of("gain_shift", 1) + of("first_rstd", 2)
         scalar += of("weigh", 0, 0) + of("weigh", 0, 1)
         scalar += of("mean", 3) + of("gain_shift", 2) + of("squares", 3) + of("first_rstd", 3)
@@ -553,8 +553,8 @@ def tile_quantuminspiredneuralcore_pb_kernel(
             for half in range(HALVES):
                 tensor += of("transpose_y", n, half) + of("products", n + 1, half)
             scalar += of("weigh", n + 1, 0) + of("weigh", n + 1, 1) + of("second_rstd", n) + of("gain_shift", n + 3)
-            vector += of("row_stats", n, 0) + of("round_hn", n + 2) + of("quantise_hn", n + 2) + of("row_stats", n, 1)
-            vector += of("finish", n - 1) + of("aggregate", n) + of("centre", n)
+            vector += of("round_hn", n + 2) + of("row_stats", n, 0) + of("quantise_hn", n + 2) + of("finish", n - 1)
+            vector += of("row_stats", n, 1) + of("aggregate", n) + of("centre", n)
         vector += of("finish", TOKEN_TILES - 1)
 
         left = write_down([vector, scalar, tensor])

@@ -30,13 +30,16 @@ PATHS = 2
 PATH_PASSES = FEATURES // K_PASS
 EPS = 1e-5
 
-BLOCKS = [
-    ("e", 0), ("e", 1), ("e", 2), ("e", 3), ("ent", 0), ("ent", 1), ("ent", 2), ("ent", 3), ("ent", 4), ("ent", 5), ("ent", 6), ("ent", 7), ("path", 0), ("path", 1), ("path", 2), ("path", 3),
-]
+BLOCKS = (
+    [("e", 0), ("ent", 0)]
+    + [("e", tt) for tt in range(1, TOKEN_TILES)]
+    + [("ent", c) for c in range(1, ENT_PASSES)]
+    + [("path", n) for n in range(PATHS * PATH_PASSES)]
+)
 RAW_BUFS = 6
 GROUPED_BUFS = 3
 
-ENT_VECTOR_COLS = 480
+ENT_VECTOR_COLS = 496
 PATH_VECTOR_COLS = 576
 
 ROUND_TO_INT = 12582912.0
@@ -500,27 +503,25 @@ def tile_quantuminspiredneuralcore_pb_kernel(
 
         first_path = block_of["path", 0]
         TILE_ORDER = [2, 3, 0, 1]
-        loads = [("load", 0), ("load_h", 0), ("load", 1), "load_ln3", ("load_h", 2), ("load", 2)]
+        e_at = [block_of["e", tt] for tt in range(TOKEN_TILES)]
+        ent_at = [block_of["ent", c] for c in range(ENT_PASSES)]
+        loads = [("load", 0), ("load_h", 0), ("load", 1), ("load", 2), "load_ln3", ("load_h", 2)]
         loads += [("load", i) for i in range(3, len(BLOCKS))] + ["load_ln4"]
         vector = ["copy_vectors"] + [("chore", n) for n in range(SINES_BEHIND + 1)]
-        vector += [("empty_e", 0, 0), ("start_x", 0), ("start_x", 1), ("quantise", 0), "copy_ln3", ("start_x", 2), ("start_x", 3), ("quantise", 1), ("quantise", 2)]
-        scalar = ["sin_table", "copy_ent_pb"]
-        for i in range(TOKEN_TILES):
-            scalar += [("empty_e", i, half) for half in range(2) if (i, half) != (0, 0)]
-            if i == 0:
-                scalar += ["sines", "norm_table"]
+        vector += [("empty_e", 0, 0), ("start_x", 0), ("start_x", 1), ("vcopy", 1), ("quantise", 0), ("start_x", 2), ("quantise", 1)]
+        vector += ["copy_ln3", ("start_x", 3), ("quantise", 2), ("quantise", 3)]
+        scalar = ["sin_table", "copy_ent_pb", ("empty_e", 0, 1), "sines", "norm_table", ("scopy", 1)]
+        scalar += [("empty_e", i, half) for i in e_at[1:] for half in range(2)]
         tensor = ["spread_ent_pb", "turn_vectors", ("transpose_e", 0, 0), ("transpose_e", 0, 1)]
-        tensor += [("transpose_e", 1, 0), ("transpose_e", 1, 1), "turn_ln3"]
-        tensor += [("transpose_e", i, half) for i in range(2, TOKEN_TILES) for half in range(2)]
-        first_ent = block_of["ent", 0]
-        for i in range(first_ent, first_path + 1):
+        tensor += [("transpose_e", e_at[1], 0), ("transpose_e", e_at[1], 1), "turn_ln3"]
+        tensor += [("transpose_e", i, half) for i in e_at[2:] for half in range(2)]
+        for n in range(1, ENT_PASSES + 1):
+            i = ent_at[n] if n < ENT_PASSES else first_path
             vector += [("vcopy", i), ("quantise", i - 1)]
             scalar.append(("scopy", i))
-            n = i - first_ent
-            if SINES_BEHIND + 1 + n < len(chores):
-                vector.append(("chore", SINES_BEHIND + 1 + n))
-            if n >= 1:
-                tensor += [("multiply", n - 1, tt) for tt in TILE_ORDER]
+            if SINES_BEHIND + n < len(chores):
+                vector.append(("chore", SINES_BEHIND + n))
+            tensor += [("multiply", n - 1, tt) for tt in TILE_ORDER]
 
         with tc.tile_pool(name="stage1", bufs=1) as stage1:
             e_codes = stage1.tile([P, TOKEN_TILES, ENT_PASSES, P], U32, align_bytes=64)

from contextlib import ExitStack
import math

import concourse.mybir as mybir
from concourse.masks import make_identity

F32 = mybir.dt.float32
BF16 = mybir.dt.bfloat16
I32 = mybir.dt.int32
U32 = mybir.dt.uint32
U8 = mybir.dt.uint8
FP8X4 = mybir.dt.float8_e4m3fn_x4
ALU = mybir.AluOpType
ACT = mybir.ActivationFunctionType

P = 128
PACK = 4
K_PASS = P * PACK
BANK = 512
RING = 4

TOKENS = 512
TOKEN_TILES = TOKENS // P
FEATURES = 1024
FEATURE_TILES = FEATURES // P
HALVES = FEATURES // BANK
K_ENT = 4096
ENT_PASSES = K_ENT // K_PASS
PATHS = 2
PATH_PASSES = FEATURES // K_PASS
EPS = 1e-5

BLOCKS = (
    [("e", 0), ("ent", 0)]
    + [("e", tt) for tt in range(1, TOKEN_TILES)]
    + [("ent", c) for c in range(1, ENT_PASSES)]
    + [("path", n) for n in range(PATHS * PATH_PASSES)]
)
RAW_BUFS = 6
GROUPED_BUFS = 3

ENT_VECTOR_COLS = 496
PATH_VECTOR_COLS = 576

ROUND_TO_INT = 12582912.0

FLOPS = 2 * TOKENS * K_ENT * FEATURES + 2 * PATHS * TOKENS * FEATURES * FEATURES


def tile_quantuminspiredneuralcore_pb_kernel(
    tc, e, h, ent_pw, ent_pb, ln3_g, ln3_b, path_w, path_b, phase, ln4_g, ln4_b, out
):
    nc = tc.nc
    e_rows = e.flatten_outer_dims()
    h_rows = h.flatten_outer_dims()
    out_rows = out.flatten_outer_dims()

    with ExitStack() as ctx:
        ctx.enter_context(tc.manual_schedule())
        consts = ctx.enter_context(tc.tile_pool(name="consts", bufs=1))
        keep = ctx.enter_context(tc.tile_pool(name="keep", bufs=1))
        stats = ctx.enter_context(tc.tile_pool(name="stats", bufs=TOKEN_TILES))
        scratch = ctx.enter_context(tc.tile_pool(name="scratch", bufs=2))
        raw_pool = ctx.enter_context(tc.tile_pool(name="raw", bufs=RAW_BUFS))
        grouped_pool = ctx.enter_context(tc.tile_pool(name="grouped", bufs=GROUPED_BUFS))
        psum = ctx.enter_context(tc.psum_pool(name="psum", bufs=RING))

        ident_f32 = consts.tile([P, P], F32)
        make_identity(nc, ident_f32[:])
        eps = consts.tile([P, 1], F32)
        nc.vector.memset(eps[:], EPS)
        ent_pb_rows = consts.tile([P, FEATURES], BF16)
        nc.vector.memset(ent_pb_rows[:].bitcast(I32), 0)
        vec_rows = consts.tile([P, FEATURES], BF16)
        nc.vector.memset(vec_rows[:].bitcast(I32), 0)
        ln3_rows = consts.tile([P, FEATURES], BF16)
        nc.vector.memset(ln3_rows[:].bitcast(I32), 0)
        ident_bf16 = consts.tile([P, P], BF16)
        nc.vector.tensor_copy(out=ident_bf16[:], in_=ident_f32[:])
        table_warm = consts.tile([P, 1], F32)

        h_sb = keep.tile([P, TOKEN_TILES, FEATURES], BF16)
        x_all = keep.tile([P, TOKEN_TILES, FEATURES], F32)
        hn_t = keep.tile([P, FEATURE_TILES, TOKENS], F32)
        hn_grouped = keep.tile([P, TOKEN_TILES, PATH_PASSES, P * PACK], BF16, align_bytes=64)
        hn_codes = keep.tile([P, TOKEN_TILES, PATH_PASSES, P], U32, align_bytes=64)
        hn_scales = keep.tile([P, TOKEN_TILES, PATH_PASSES, P], U8, align_bytes=64)
        w2_codes = keep.tile([P, PATHS, PATH_PASSES, FEATURES], U32, align_bytes=64)
        w2_scales = keep.tile([P, PATHS, PATH_PASSES, FEATURES], U8, align_bytes=64)
        ln4_g_spread = consts.tile([P, FEATURES], BF16)
        ln4_b_spread = consts.tile([P, FEATURES], BF16)
        ent_pb_spread = consts.tile([P, FEATURES], BF16)
        vec_cols = consts.tile([P, 2 * PATHS, FEATURE_TILES], F32)
        path_b_cols, phase_cols = vec_cols[:, 0:PATHS, :], vec_cols[:, PATHS : 2 * PATHS, :]
        ln3_cols = consts.tile([P, 2, FEATURE_TILES], F32)
        ln3_g_cols, ln3_b_cols = ln3_cols[:, 0, :], ln3_cols[:, 1, :]
        turns = consts.tile([P, PATHS, FEATURE_TILES], F32)
        angle = consts.tile([P, PATHS, FEATURE_TILES], F32)
        sin_full = consts.tile([P, PATHS, FEATURE_TILES], F32)
        sin_half = consts.tile([P, PATHS, FEATURE_TILES], F32)
        mod = consts.tile([P, PATHS, FEATURE_TILES], F32)
        bias_mod = consts.tile([P, PATHS, FEATURE_TILES], F32)
        bias_sum = consts.tile([P, FEATURE_TILES], F32)

        tasks = {}
        done = set()
        raw, grouped, memory = {}, {}, {}
        emptied_by = {"left": [], "right": []}

        def bank(ring, shape, dtype, reader):
            emptied_by[ring].append(reader)
            return psum.tile(shape, dtype, tag=ring, name=ring + "_bank")

        def banks_free(ring, count):
            return all(r in done for r in emptied_by[ring][-RING:][:max(0, count - max(0, RING - len(emptied_by[ring])))])

        def weight_rows(kind, index):
            if kind == "ent":
                chunk = ent_pw[index * K_PASS : (index + 1) * K_PASS, :]
                return chunk.rearrange("(u p s) n -> p u (s n)", u=2, s=2)
            path, c = divmod(index, PATH_PASSES)
            return path_w[path, c * K_PASS : (c + 1) * K_PASS, :].rearrange("(t p) n -> p t n", p=P)

        def load(i):
            kind, index = BLOCKS[i]
            raw[i] = raw_pool.tile([P, K_ENT], BF16, tag="raw", name="raw")
            if kind == "e":
                parts = 2 if index == 0 else 1
                for part in range(parts):
                    cols = slice(part * (K_ENT // parts), (part + 1) * (K_ENT // parts))
                    nc.sync.dma_start(out=raw[i][:, cols], in_=e_rows[index * P : (index + 1) * P, cols])
                    if index == 0 and part == 0:
                        load_vectors()
            else:
                rows = weight_rows(kind, index)
                nc.sync.dma_start(out=raw[i][:].rearrange("p (a b) -> p a b", a=rows.shape[1]), in_=rows)

        def load_h(tt):
            rows = h_rows[tt * P : (tt + 2) * P, :].rearrange("(t p) f -> p t f", p=P)
            nc.sync.dma_start(out=h_sb[:, tt : tt + 2, :], in_=rows)

        def load_vectors():
            nc.sync.dma_start(out=ent_pb_rows[0:1, :], in_=ent_pb.unsqueeze(0))
            nc.sync.dma_start(out=vec_rows[PATHS : 2 * PATHS, :], in_=phase)
            nc.sync.dma_start(out=vec_rows[0:PATHS, :], in_=path_b)

        def load_ln3():
            nc.sync.dma_start(out=ln3_rows[0:1, :], in_=ln3_g.unsqueeze(0))
            nc.sync.dma_start(out=ln3_rows[1:2, :], in_=ln3_b.unsqueeze(0))

        def load_ln4():
            nc.sync.dma_start(out=ln4_g_spread[:], in_=ln4_g.partition_broadcast(P))
            nc.sync.dma_start(out=ln4_b_spread[:], in_=ln4_b.partition_broadcast(P))

        def grouped_tile(i):
            for k in range(len(grouped), i + 1):
                grouped[k] = grouped_pool.tile([P, K_ENT], BF16, tag="grouped", name="grouped", align_bytes=64)
            return grouped[i]

        def transpose_e(i, half):
            e_words = raw[i][:].bitcast(F32)
            for pair in (2 * half, 2 * half + 1):
                e_bank = bank("right", [P, 2, 2, P], F32, ("empty_e", i, half))
                for c2 in range(2):
                    for u in range(2):
                        first = (2 * pair + c2) * 2 * P + u * P
                        nc.tensor.transpose(e_bank[:, c2, u, :], e_words[:, first : first + P], ident_f32[:])
                memory["e", i, pair] = e_bank

        def empty_e(i, half):
            grouped_words = grouped_tile(i)[:].bitcast(F32).rearrange("p (c r u) -> p c r u", c=ENT_PASSES, u=2)
            for pair in (2 * half, 2 * half + 1):
                copy = nc.vector.tensor_copy if (i, half) == (0, 0) else nc.scalar.copy
                copy(
                    out=grouped_words[:, 2 * pair : 2 * pair + 2],
                    in_=memory["e", i, pair][:].rearrange("p c u r -> p c r u"),
                )

        def regroup(i, copy, first, last):
            src = raw[i][:].rearrange("p (t c i) -> p c t i", t=PACK, i=4)
            dst = grouped_tile(i)[:].rearrange("p (c i t) -> p c t i", i=4, t=PACK)
            copy(out=dst[:, first // 4 : last // 4], in_=src[:, first // 4 : last // 4])

        def vector_cols(i):
            kind, index = BLOCKS[i]
            if kind == "path":
                return PATH_VECTOR_COLS
            return ENT_VECTOR_COLS

        def quantise(i):
            kind, index = BLOCKS[i]
            if kind == "e":
                codes = e_codes[:, index].rearrange("p c r -> p (c r)")
                scales = e_scales[:, index].rearrange("p c r -> p (c r)")
            elif kind == "ent":
                codes, scales = w1_codes[:, index, :], w1_scales[:, index, :]
            else:
                path, c = divmod(index, PATH_PASSES)
                codes, scales = w2_codes[:, path, c, :], w2_scales[:, path, c, :]
            nc.vector.quantize_mx(out=codes.bitcast(FP8X4), scales=scales, in_=grouped[i][:])

        def multiply(c, tt):
            if ("acc", tt) not in memory:
                ring = "left" if tt < TOKEN_TILES // 2 else "right"
                memory["acc", tt] = [bank(ring, [P, BANK], F32, ("add_ent", tt)) for half in range(HALVES)]
            for half in range(HALVES):
                cols = slice(half * BANK, (half + 1) * BANK)
                nc.tensor.matmul_mx(
                    out=memory["acc", tt][half][:],
                    lhsT=e_codes[:, tt, c, :].bitcast(FP8X4),
                    lhsT_scale=e_scales[:, tt, c, :],
                    rhs=w1_codes[:, c, cols].bitcast(FP8X4),
                    rhs_scale=w1_scales[:, c, cols],
                    start=(c == 0),
                    stop=(c == ENT_PASSES - 1),
                )

        def spread_ent_pb():
            pick_row = ident_bf16[:, 0:1].to_broadcast([P, P])
            memory["pb"] = bank("right", [P, FEATURES], BF16, "copy_ent_pb")
            for half in range(HALVES):
                cols = slice(half * BANK, (half + 1) * BANK)
                nc.tensor.matmul(out=memory["pb"][:, cols], lhsT=pick_row, rhs=ent_pb_rows[:, cols], start=True, stop=True)

        def copy_ent_pb():
            nc.scalar.copy(out=ent_pb_spread[:], in_=memory["pb"][:])

        def turn_vectors():
            memory["cols"] = bank("right", [P, FEATURE_TILES, P], BF16, "copy_vectors")
            for j in range(FEATURE_TILES):
                nc.tensor.transpose(memory["cols"][:, j, :], vec_rows[:, j * P : (j + 1) * P], ident_bf16[:])

        def copy_vectors():
            nc.vector.tensor_copy(out=vec_cols[:], in_=memory["cols"][:, :, 0 : 2 * PATHS].rearrange("p j r -> p r j"))

        def turn_ln3():
            memory["ln3"] = bank("right", [P, FEATURE_TILES, P], BF16, "copy_ln3")
            for j in range(FEATURE_TILES):
                nc.tensor.transpose(memory["ln3"][:, j, :], ln3_rows[:, j * P : (j + 1) * P], ident_bf16[:])

        def copy_ln3():
            nc.vector.tensor_copy(out=ln3_cols[:], in_=memory["ln3"][:, :, 0:2].rearrange("p j r -> p r j"))

        def sines():
            nc.scalar.activation(out=sin_full[:], in_=angle[:], func=ACT.Sin)
            nc.scalar.activation(out=sin_half[:], in_=angle[:], func=ACT.Sin, scale=0.5)

        chores = [
            lambda: nc.vector.tensor_scalar(
                out=turns[:], in0=phase_cols, scalar1=1.0 / (2.0 * math.pi), scalar2=ROUND_TO_INT,
                op0=ALU.mult, op1=ALU.add,
            ),
            lambda: nc.vector.tensor_scalar(
                out=turns[:], in0=turns[:], scalar1=ROUND_TO_INT, scalar2=None, op0=ALU.subtract
            ),
            lambda: nc.vector.scalar_tensor_tensor(
                out=angle[:], in0=turns[:], scalar=-2.0 * math.pi, in1=phase_cols, op0=ALU.mult, op1=ALU.add
            ),
            lambda: nc.vector.tensor_tensor(out=mod[:], in0=sin_half[:], in1=sin_half[:], op=ALU.mult),
            lambda: nc.vector.tensor_scalar(
                out=mod[:], in0=mod[:], scalar1=-2.0, scalar2=1.0, op0=ALU.mult, op1=ALU.add
            ),
            lambda: nc.vector.tensor_tensor(out=mod[:], in0=mod[:], in1=sin_full[:], op=ALU.add),
            lambda: nc.vector.tensor_tensor(out=bias_mod[:], in0=path_b_cols, in1=mod[:], op=ALU.mult),
            lambda: nc.vector.tensor_tensor(out=bias_sum[:], in0=bias_mod[:, 0, :], in1=bias_mod[:, 1, :], op=ALU.add),
        ]
        SINES_BEHIND = 2

        def start_x(tt):
            nc.vector.tensor_tensor(out=x_all[:, tt, :], in0=h_sb[:, tt, :], in1=ent_pb_spread[:], op=ALU.add)

        def add_ent(tt):
            memory["sums", tt] = stats.tile([P, HALVES], F32, name="row_sums")
            for half in range(HALVES):
                cols = slice(half * BANK, (half + 1) * BANK)
                nc.vector.scalar_tensor_tensor(
                    out=x_all[:, tt, cols], in0=memory["acc", tt][half][:], scalar=0.0, in1=x_all[:, tt, cols],
                    op0=ALU.add, op1=ALU.add, accum_out=memory["sums", tt][:, half : half + 1],
                )

        def mean(tt):
            scaled_sums = stats.tile([P, HALVES], F32, name="scaled_sums")
            memory["neg_mean", tt] = stats.tile([P, 1], F32, name="neg_mean")
            nc.scalar.activation(
                out=scaled_sums[:], in_=memory["sums", tt][:], func=ACT.Identity, scale=-1.0 / FEATURES,
                accum_out=memory["neg_mean", tt][:],
            )

        def squares(tt):
            squared = scratch.tile([P, FEATURES], BF16, name="squared")
            memory["sum_sq", tt] = stats.tile([P, 1], F32, name="sum_sq")
            nc.scalar.activation(
                out=squared[:], in_=x_all[:, tt, :], func=ACT.Square, bias=memory["neg_mean", tt][:], scale=1.0,
                accum_out=memory["sum_sq", tt][:],
            )

        def first_rstd(tt):
            memory["rstd", tt] = stats.tile([P, 1], F32, name="rstd")
            nc.scalar.activation(
                out=memory["rstd", tt][:], in_=memory["sum_sq", tt][:], func=ACT.Abs_reciprocal_sqrt, bias=eps[:],
                scale=1.0 / FEATURES,
            )

        def normalise(tt):
            nc.vector.tensor_scalar(
                out=x_all[:, tt, :], in0=x_all[:, tt, :], scalar1=memory["neg_mean", tt][:],
                scalar2=memory["rstd", tt][:], op0=ALU.add, op1=ALU.mult,
            )

        def transpose_z(tt):
            memory["z", tt] = []
            for c in range(PATH_PASSES):
                z_bank = bank("right", [P, PACK, P], F32, ("gain_shift", tt))
                for t in range(PACK):
                    first = c * K_PASS + t * P
                    nc.tensor.transpose(z_bank[:, t, :], x_all[:, tt, first : first + P], ident_f32[:])
                memory["z", tt].append(z_bank)

        def gain_shift(tt):
            tokens = slice(tt * P, (tt + 1) * P)
            for j in range(FEATURE_TILES):
                c, t = divmod(j, PACK)
                nc.scalar.activation(
                    out=hn_t[:, j, tokens], in_=memory["z", tt][c][:, t, :], func=ACT.Identity,
                    scale=ln3_g_cols[:, j : j + 1], bias=ln3_b_cols[:, j : j + 1],
                )

        def round_hn(tt):
            tokens = slice(tt * P, (tt + 1) * P)
            for c in range(PATH_PASSES):
                nc.vector.tensor_copy(
                    out=hn_grouped[:, tt, c].rearrange("p (q i t) -> p q t i", i=4, t=PACK),
                    in_=hn_t[:, c * PACK : (c + 1) * PACK, tokens].rearrange("p t (q i) -> p q t i", i=4),
                )

        def quantise_hn(tt):
            nc.vector.quantize_mx(
                out=hn_codes[:, tt].rearrange("p c r -> p (c r)").bitcast(FP8X4),
                scales=hn_scales[:, tt].rearrange("p c r -> p (c r)"),
                in_=hn_grouped[:, tt].rearrange("p c w -> p (c w)"),
            )

        def products(tt, path):
            for quad in range(FEATURE_TILES // 4):
                t_bank = bank("right", [P, 4, P], F32, ("weigh", tt, path))
                memory["t", tt, path, quad] = t_bank
                for k in range(4):
                    feats = slice((4 * quad + k) * P, (4 * quad + k + 1) * P)
                    for c in range(PATH_PASSES):
                        nc.tensor.matmul_mx(
                            out=t_bank[:, k, :],
                            lhsT=w2_codes[:, path, c, feats].bitcast(FP8X4),
                            lhsT_scale=w2_scales[:, path, c, feats],
                            rhs=hn_codes[:, tt, c, :].bitcast(FP8X4),
                            rhs_scale=hn_scales[:, tt, c, :],
                            start=(c == 0),
                            stop=(c == PATH_PASSES - 1),
                        )

        def weigh(tt, path):
            tokens = slice(tt * P, (tt + 1) * P)
            for j in range(FEATURE_TILES):
                quad, k = divmod(j, 4)
                nc.scalar.activation(
                    out=interf_t[:, path, j, tokens], in_=memory["t", tt, path, quad][:, k, :], func=ACT.Identity,
                    scale=mod[:, path, j : j + 1], bias=bias_sum[:, j : j + 1] if path == 0 else 0.0,
                )

        def transpose_y(tt, half):
            tokens = slice(tt * P, (tt + 1) * P)
            y_bank = bank("left", [P, BANK], F32, ("centre", tt))
            memory["y", tt, half] = y_bank
            for q in range(BANK // P):
                j = half * (BANK // P) + q
                terms = [hn_t[:, j, tokens], interf_t[:, 0, j, tokens], interf_t[:, 1, j, tokens]]
                for n, term in enumerate(terms):
                    nc.tensor.matmul(
                        out=y_bank[:, q * P : (q + 1) * P], lhsT=term, rhs=ident_f32[:],
                        is_transpose=True, start=(n == 0), stop=(n == len(terms) - 1),
                    )

        def row_statistics(tt, half):
            if half == 0:
                memory["parts", tt] = stats.tile([P, HALVES, 6], F32, name="parts")
            nc.vector.bn_stats(out=memory["parts", tt][:, half, :], in_=memory["y", tt, half][:])

        def aggregate(tt):
            memory["mean_var", tt] = stats.tile([P, 2], F32, name="mean_var")
            nc.vector.bn_aggr(out=memory["mean_var", tt][:], in_=memory["parts", tt][:].rearrange("p h s -> p (h s)"))

        def second_rstd(tt):
            memory["rstd2", tt] = stats.tile([P, 1], F32, name="rstd2")
            nc.scalar.activation(
                out=memory["rstd2", tt][:], in_=memory["mean_var", tt][:, 1:2], func=ACT.Abs_reciprocal_sqrt,
                bias=eps[:], scale=1.0,
            )

        def centre(tt):
            for half in range(HALVES):
                cols = slice(half * BANK, (half + 1) * BANK)
                nc.vector.scalar_tensor_tensor(
                    out=x_all[:, tt, cols], in0=memory["y", tt, half][:], scalar=memory["mean_var", tt][:, 0:1],
                    in1=ln4_g_spread[:, cols], op0=ALU.subtract, op1=ALU.mult,
                )

        def finish(tt):
            for half in range(HALVES):
                cols = slice(half * BANK, (half + 1) * BANK)
                nc.vector.scalar_tensor_tensor(
                    out=x_all[:, tt, cols], in0=x_all[:, tt, cols], scalar=memory["rstd2", tt][:],
                    in1=ln4_b_spread[:, cols], op0=ALU.mult, op1=ALU.add,
                )
                nc.sync.dma_start(out=out_rows[tt * P : (tt + 1) * P, cols], in_=x_all[:, tt, cols])

        block_of = {b: i for i, b in enumerate(BLOCKS)}

        def task(name, needs, write, banks=None):
            tasks[name] = (needs, write, banks)

        for i, (kind, index) in enumerate(BLOCKS):
            before = i - RAW_BUFS
            freed = []
            if before >= 0:
                freed = [("transpose_e", before, 0), ("transpose_e", before, 1)] if BLOCKS[before][0] == "e" else [("vcopy", before), ("scopy", before)]
            task(("load", i), freed, lambda i=i: load(i))
            reuse = [("quantise", i - GROUPED_BUFS)] if i >= GROUPED_BUFS else []
            if kind == "e":
                for half in range(2):
                    task(("transpose_e", i, half), [("load", i)], lambda i=i, half=half: transpose_e(i, half), ("right", 2))
                    task(("empty_e", i, half), [("transpose_e", i, half)] + reuse, lambda i=i, half=half: empty_e(i, half))
                task(("quantise", i), [("empty_e", i, 0), ("empty_e", i, 1)], lambda i=i: quantise(i))
            else:
                split = vector_cols(i)
                task(("vcopy", i), [("load", i)] + reuse, lambda i=i, s=split: regroup(i, nc.vector.tensor_copy, 0, s) if s > 0 else None)
                task(("scopy", i), [("load", i)] + reuse, lambda i=i, s=split: regroup(i, nc.scalar.copy, s, FEATURES) if s < FEATURES else None)
                task(("quantise", i), [("vcopy", i), ("scopy", i)], lambda i=i: quantise(i))
        last_e = max(i for i, b in enumerate(BLOCKS) if b[0] == "e")
        for tt in range(TOKEN_TILES):
            if tt % 2 == 0:
                task(("load_h", tt), [], lambda tt=tt: load_h(tt))
            for c in range(ENT_PASSES):
                needs = [("quantise", block_of["e", tt]), ("quantise", block_of["ent", c])]
                if tt >= TOKEN_TILES // 2:
                    needs += [("empty_e", last_e, 1), "copy_ent_pb", "copy_vectors", "copy_ln3"]
                task(("multiply", c, tt), needs, lambda c=c, tt=tt: multiply(c, tt),
                     ("left" if tt < TOKEN_TILES // 2 else "right", 2) if c == 0 else None)
            task(("start_x", tt), [("load_h", tt - tt % 2), "copy_ent_pb"], lambda tt=tt: start_x(tt))
            task(("add_ent", tt), [("start_x", tt)] + [("multiply", c, tt) for c in range(ENT_PASSES)], lambda tt=tt: add_ent(tt))
            task(("mean", tt), [("add_ent", tt)], lambda tt=tt: mean(tt))
            task(("squares", tt), [("mean", tt)], lambda tt=tt: squares(tt))
            task(("first_rstd", tt), [("squares", tt)], lambda tt=tt: first_rstd(tt))
            task(("normalise", tt), [("first_rstd", tt)], lambda tt=tt: normalise(tt))
            task(("transpose_z", tt), [("normalise", tt)], lambda tt=tt: transpose_z(tt), ("right", 2))
            task(("gain_shift", tt), [("transpose_z", tt), "copy_ln3"], lambda tt=tt: gain_shift(tt))
            task(("round_hn", tt), [("gain_shift", tt)], lambda tt=tt: round_hn(tt))
            task(("quantise_hn", tt), [("round_hn", tt)], lambda tt=tt: quantise_hn(tt))
            for path in range(PATHS):
                chunks = [block_of["path", path * PATH_PASSES + c] for c in range(PATH_PASSES)]
                task(("products", tt, path), [("quantise_hn", tt)] + [("quantise", i) for i in chunks],
                     lambda tt=tt, path=path: products(tt, path), ("right", 2))
                task(("weigh", tt, path), [("products", tt, path), ("chore", len(chores) - 1)], lambda tt=tt, path=path: weigh(tt, path))
            for half in range(HALVES):
                task(("transpose_y", tt, half), [("weigh", tt, 0), ("weigh", tt, 1)], lambda tt=tt, half=half: transpose_y(tt, half), ("left", 1))
                task(("row_stats", tt, half), [("transpose_y", tt, half)] + ([("row_stats", tt, 0)] if half else []), lambda tt=tt, half=half: row_statistics(tt, half))
            task(("aggregate", tt), [("row_stats", tt, 0), ("row_stats", tt, 1)], lambda tt=tt: aggregate(tt))
            task(("second_rstd", tt), [("aggregate", tt)], lambda tt=tt: second_rstd(tt))
            task(("centre", tt), [("aggregate", tt), "load_ln4"], lambda tt=tt: centre(tt))
            task(("finish", tt), [("centre", tt), ("second_rstd", tt)], lambda tt=tt: finish(tt))
        task("sin_table", [], lambda: nc.scalar.activation(out=table_warm[:], in_=eps[:], func=ACT.Sin))
        task("load_ln4", [], load_ln4)
        task("spread_ent_pb", [("load", 0)], spread_ent_pb, ("right", 1))
        task("copy_ent_pb", ["spread_ent_pb"], copy_ent_pb)
        task("turn_vectors", [("load", 0)], turn_vectors, ("right", 1))
        task("copy_vectors", ["turn_vectors"], copy_vectors)
        task("load_ln3", [], load_ln3)
        task("turn_ln3", ["load_ln3"], turn_ln3, ("right", 1))
        task("copy_ln3", ["turn_ln3"], copy_ln3)
        for n, chore in enumerate(chores):
            needs = ["copy_vectors"] if n == 0 else [("chore", n - 1)]
            if n == SINES_BEHIND + 1:
                needs.append("sines")
            task(("chore", n), needs, chore)
        task("sines", [("chore", SINES_BEHIND)], sines)
        task("norm_table", ["sines"], lambda: nc.scalar.activation(
            out=table_warm[:], in_=sin_half[:, 0, 0:1], func=ACT.Abs_reciprocal_sqrt, bias=eps[:], scale=0.0))


        def write_down(queues):
            heads = [0 for q in queues]
            moved = True
            while moved:
                moved = False
                for k, queue in enumerate(queues):
                    while heads[k] < len(queue):
                        needs, write, banks = tasks[queue[heads[k]]]
                        if not all(n in done for n in needs) or (banks is not None and not banks_free(banks[0], banks[1])):
                            break
                        write()
                        done.add(queue[heads[k]])
                        heads[k] += 1
                        moved = True
            return [q[n:] for q, n in zip(queues, heads)]

        first_path = block_of["path", 0]
        TILE_ORDER = [2, 3, 0, 1]
        e_at = [block_of["e", tt] for tt in range(TOKEN_TILES)]
        ent_at = [block_of["ent", c] for c in range(ENT_PASSES)]
        loads = [("load", 0), ("load_h", 0), ("load", 1), ("load", 2), "load_ln3", ("load_h", 2)]
        loads += [("load", i) for i in range(3, len(BLOCKS))] + ["load_ln4"]
        vector = ["copy_vectors"] + [("chore", n) for n in range(SINES_BEHIND + 1)]
        vector += [("empty_e", 0, 0), ("start_x", 0), ("start_x", 1), ("vcopy", 1), ("quantise", 0), ("start_x", 2), ("quantise", 1)]
        vector += ["copy_ln3", ("start_x", 3), ("quantise", 2), ("quantise", 3)]
        scalar = ["sin_table", "copy_ent_pb", ("empty_e", 0, 1), "sines", "norm_table", ("scopy", 1)]
        scalar += [("empty_e", i, half) for i in e_at[1:] for half in range(2)]
        tensor = ["spread_ent_pb", "turn_vectors", ("transpose_e", 0, 0), ("transpose_e", 0, 1)]
        tensor += [("transpose_e", e_at[1], 0), ("transpose_e", e_at[1], 1), "turn_ln3"]
        tensor += [("transpose_e", i, half) for i in e_at[2:] for half in range(2)]
        for n in range(1, ENT_PASSES + 1):
            i = ent_at[n] if n < ENT_PASSES else first_path
            vector += [("vcopy", i), ("quantise", i - 1)]
            scalar.append(("scopy", i))
            if SINES_BEHIND + n < len(chores):
                vector.append(("chore", SINES_BEHIND + n))
            tensor += [("multiply", n - 1, tt) for tt in TILE_ORDER]

        with tc.tile_pool(name="stage1", bufs=1) as stage1:
            e_codes = stage1.tile([P, TOKEN_TILES, ENT_PASSES, P], U32, align_bytes=64)
            e_scales = stage1.tile([P, TOKEN_TILES, ENT_PASSES, P], U8, align_bytes=64)
            w1_codes = stage1.tile([P, ENT_PASSES, FEATURES], U32, align_bytes=64)
            w1_scales = stage1.tile([P, ENT_PASSES, FEATURES], U8, align_bytes=64)
            left = write_down([loads, vector, scalar, tensor])
        assert not any(left), left
        tail = ctx.enter_context(tc.tile_pool(name="tail", bufs=1))
        interf_t = tail.tile([P, PATHS, FEATURE_TILES, TOKENS], F32)

        def of(stage, n, *rest):
            return [(stage, TILE_ORDER[n]) + rest] if 0 <= n < TOKEN_TILES else []

        def chunk(stage, n):
            return [(stage, first_path + n)]

        vector = chunk("vcopy", 1) + of("add_ent", 0) + of("add_ent", 1) + chunk("quantise", 0) + of("normalise", 0)
        vector += chunk("vcopy", 2) + of("add_ent", 2) + of("normalise", 1) + chunk("quantise", 1) + of("round_hn", 0)
        vector += chunk("vcopy", 3) + of("quantise_hn", 0) + chunk("quantise", 2) + chunk("quantise", 3)
        vector += of("normalise", 2) + of("add_ent", 3) + of("round_hn", 1) + of("quantise_hn", 1) + of("normalise", 3)
        scalar = chunk("scopy", 1) + of("mean", 0) + of("squares", 0) + of("mean", 1) + of("first_rstd", 0) + of("squares", 1)
        scalar += of("first_rstd", 1) + chunk("scopy", 2) + of("gain_shift", 0) + of("mean", 2)
        scalar += chunk("scopy", 3) + of("squares", 2) + of("gain_shift", 1) + of("first_rstd", 2)
        scalar += of("weigh", 0, 0) + of("weigh", 0, 1)
        scalar += of("mean", 3) + of("gain_shift", 2) + of("squares", 3) + of("first_rstd", 3)
        tensor = of("transpose_z", 0) + of("transpose_z", 1) + of("products", 0, 0) + of("products", 0, 1)
        for n in range(TOKEN_TILES):
            tensor += of("transpose_z", n + 2)
            for half in range(HALVES):
                tensor += of("transpose_y", n, half) + of("products", n + 1, half)
            scalar += of("weigh", n + 1, 0) + of("weigh", n + 1, 1) + of("second_rstd", n) + of("gain_shift", n + 3)
            vector += of("round_hn", n + 2) + of("row_stats", n, 0) + of("quantise_hn", n + 2) + of("finish", n - 1)
            vector += of("row_stats", n, 1) + of("aggregate", n) + of("centre", n)
        vector += of("finish", TOKEN_TILES - 1)

        left = write_down([vector, scalar, tensor])
        assert not any(left), left
